import numpy as np
import ml_dtypes


def mxq(x, axis, fmt="e4m3"):
    dtype, down = {"e4m3": (ml_dtypes.float8_e4m3fn, 7), "e5m2": (ml_dtypes.float8_e5m2, 14)}[fmt]
    v = np.moveaxis(np.asarray(x, np.float32).astype(ml_dtypes.bfloat16).astype(np.float64), axis, -1)
    blocks = v.reshape(v.shape[:-1] + (-1, 32))
    amax = np.abs(blocks).max(-1, keepdims=True)
    byte = np.maximum(np.where(amax > 0, np.frexp(amax)[1] - 1 + 127, 0) - down, 1)
    scale = np.exp2(byte - 127.0)
    codes = (blocks / scale).astype(np.float32).astype(dtype).astype(np.float64)
    return np.moveaxis((codes * scale).reshape(v.shape), -1, axis)


WIDE = False


def mx_kscale(k):
    if not WIDE:
        return np.ones(k)
    levels = np.array([10, -10, 5, -5, 0])
    a = np.random.permutation(np.resize(levels, k // 512 * 4)).reshape(k // 512, 4)
    idx = np.arange(k)
    return np.exp2(a[idx // 512, idx % 128 // 32])


BF16 = ml_dtypes.bfloat16


def bf(x):
    return np.asarray(x, np.float32).astype(BF16)


def f64(x):
    return np.asarray(x).astype(np.float64)


E2M1 = np.array([0.0, 0.5, 1.0, 1.5, 2.0, 3.0, 4.0, 6.0, -0.0, -0.5, -1.0, -1.5, -2.0, -3.0, -4.0, -6.0])


def pack_weight(w, fmt):
    k, n = w.shape
    w = f64(bf(w)).reshape(k // 32, 32, n)
    amax = np.abs(w).max(1)
    if fmt == "e4m3":
        byte = np.frexp(amax)[1] - 1 + 127 - 7
    else:
        mant, ex = np.frexp(amax / 6.0)
        byte = np.where(mant > 0.5, ex, ex - 1) + 127
    byte = np.clip(np.where(amax > 0, byte, 1), 1, 254)
    scaled = (w * np.exp2(127.0 - byte)[:, None, :]).reshape(k, n).astype(np.float32)
    by_word = np.ascontiguousarray(scaled.reshape(k // 512, 128, 4, n).transpose(0, 1, 3, 2))
    if fmt == "e4m3":
        words = by_word.astype(ml_dtypes.float8_e4m3fn).view(np.uint8)
    else:
        c = by_word.astype(ml_dtypes.float4_e2m1fn).view(np.uint8) & 0xF
        words = c[..., 0::2] | (c[..., 1::2] << 4)
    return np.ascontiguousarray(words), np.ascontiguousarray(byte.astype(np.uint8).reshape(k // 512, 16, n))


def unpack_weight(words, scales, fmt):
    g, p, n, _ = words.shape
    if fmt == "e4m3":
        vals = np.ascontiguousarray(words).view(ml_dtypes.float8_e4m3fn).astype(np.float64)
    else:
        nib = np.empty((g, p, n, 4), np.uint8)
        nib[..., 0::2] = words & 0xF
        nib[..., 1::2] = words >> 4
        vals = E2M1[nib]
    vals = vals * np.repeat(np.exp2(scales.astype(np.float64) - 127.0), 8, axis=1)[..., None]
    return vals.transpose(0, 1, 3, 2).reshape(g * 512, n)

def pack4(w):
    words, scales = pack_weight(w, "e2m1")
    return words.reshape(words.shape[0], 128, -1), scales


def unpack4(words, scales):
    return unpack_weight(words.reshape(words.shape[0], 128, -1, 2), scales, "e2m1")


B, CIN, H, W, CR, COUT, SP, K = 2, 1024, 8, 8, 512, 1024, 8, 7
PAD = K // 2
KK = K * K
HN = COUT // SP
HW = H * W
OFFS = [(dy, dx) for dy in range(K) for dx in range(K)]


def setup_inputs():
    s = mx_kscale(CIN)
    logits = bf(np.random.standard_normal((B, HN, KK, HW)) * 1.5)
    x = bf(np.random.standard_normal((B, CIN, H, W)) * s[None, :, None, None])
    w3c = np.random.standard_normal((COUT, CIN)) * 2.0 / np.sqrt(CIN) / s[None, :]
    b3c = bf(np.random.standard_normal(COUT) * 0.5)
    words, scales = pack4(np.ascontiguousarray(w3c.T))
    return {
        "logits": logits,
        "x": x,
        "w3c_words": words,
        "w3c_scales": scales,
        "b3c": b3c,
    }


def reference(logits, x, w3c_words, w3c_scales, b3c):
    x3 = (unpack4(w3c_words, w3c_scales).T @ mxq(f64(x).reshape(B, CIN, HW), 1, "e4m3")) + f64(b3c)[None, :, None]
    x3 = x3.reshape(B, COUT, H, W)
    lg = f64(logits)
    e = np.exp(lg - lg.max(axis=2, keepdims=True))
    wgt = (e / e.sum(axis=2, keepdims=True)).reshape(B, HN, KK, H, W)
    x3p = np.pad(x3, ((0, 0), (0, 0), (PAD, PAD), (PAD, PAD)), mode="reflect")
    acc = np.zeros((B, HN, SP, H, W))
    for k, (dy, dx) in enumerate(OFFS):
        patch = x3p[:, :, dy:dy + H, dx:dx + W].reshape(B, HN, SP, H, W)
        acc = acc + patch * wgt[:, :, k][:, :, None]
    return acc.reshape(B, COUT, H, W)

@@ -1,0 +1,235 @@
+from contextlib import ExitStack
+
+import concourse.mybir as mybir
+from concourse.masks import make_identity
+
+F32 = mybir.dt.float32
+BF16 = mybir.dt.bfloat16
+U8 = mybir.dt.uint8
+U32 = mybir.dt.uint32
+I32 = mybir.dt.int32
+FP8X4 = mybir.dt.float8_e4m3fn_x4
+FP4X4 = mybir.dt.float4_e2m1fn_x4
+ALU = mybir.AluOpType
+ACT = mybir.ActivationFunctionType
+
+P = 128
+B = 2
+CIN = 1024
+COUT = 1024
+SIDE = 8
+HW = SIDE * SIDE
+SP = 8
+HEADS = COUT // SP
+WIN = 7
+TAPS = WIN * WIN
+PAD = WIN // 2
+WIDE = SIDE + 2 * PAD
+PACK = 4
+K_PASS = P * PACK
+PASSES = CIN // K_PASS
+N_HALF = 512
+HALVES = COUT // N_HALF
+ROWS_PER_BANK = 4
+
+FLOPS = 2 * B * HW * CIN * COUT + 2 * B * COUT * HW * TAPS
+
+
+def valid_rows(dy):
+    return max(0, PAD - dy), min(SIDE, SIDE + PAD - dy)
+
+
+def reflected_tap(dy, i):
+    u = i + dy - PAD
+    source = -u if u < 0 else 2 * (SIDE - 1) - u
+    return source - i + PAD
+
+
+def tile_sam_pb_s_kernel(tc, logits, x, w3c_words, w3c_scales, b3c, out):
+    nc = tc.nc
+    with ExitStack() as ctx:
+        keep = ctx.enter_context(tc.tile_pool(name="keep", bufs=1))
+        shifted_pool = ctx.enter_context(tc.tile_pool(name="shifted", bufs=3))
+        prod_pool = ctx.enter_context(tc.tile_pool(name="prod", bufs=4))
+        psum = ctx.enter_context(tc.psum_pool(name="psum", bufs=1))
+
+        ident = keep.tile([P, P], F32)
+        make_identity(nc, ident[:])
+        w_scales = keep.tile([P, PASSES, COUT], U8, align_bytes=64)
+        nc.vector.memset(w_scales[:].bitcast(I32), 0)
+
+        x_raw = keep.tile([P, B, PASSES, PACK, HW], BF16)
+        nc.sync.dma_start(
+            out=x_raw[:].rearrange("p b g t n -> p b g (t n)"),
+            in_=x.rearrange("b (g p t) i j -> p b g (t i j)", g=PASSES, p=P, t=PACK),
+        )
+        w_words = keep.tile([P, PASSES, 2 * COUT], U8, align_bytes=64)
+        nc.sync.dma_start(
+            out=w_words[:].bitcast(I32),
+            in_=w3c_words.bitcast(I32).rearrange("g p w -> p g w"),
+        )
+        for quad in range(4):
+            nc.sync.dma_start(
+                out=w_scales[32 * quad : 32 * quad + 4].bitcast(I32),
+                in_=w3c_scales[:, 4 * quad : 4 * quad + 4, :].bitcast(I32).rearrange("g r n -> r g n"),
+            )
+        bias = keep.tile([P, SP], BF16)
+        nc.sync.dma_start(out=bias[:], in_=b3c.rearrange("(h s) -> h s", s=SP))
+        lg = keep.tile([P, B, TAPS, HW], BF16)
+        for b in range(B):
+            nc.sync.dma_start(
+                out=lg[:, b].rearrange("p l n -> p (l n)"),
+                in_=logits[b].rearrange("h l n -> h (l n)"),
+            )
+
+        grouped = keep.tile([P, PASSES, B, HW, PACK], BF16, align_bytes=64)
+        for g in range(PASSES):
+            nc.scalar.copy(out=grouped[:, g], in_=x_raw[:, :, g].rearrange("p b t n -> p b n t"))
+        x_codes = keep.tile([P, PASSES * P], U32, align_bytes=64)
+        x_scales = keep.tile([P, PASSES * P], U8, align_bytes=64)
+        nc.vector.quantize_mx(
+            out=x_codes[:].bitcast(FP8X4),
+            scales=x_scales[:],
+            in_=grouped[:].rearrange("p g b n t -> p (g b n t)"),
+        )
+        x3_pos = keep.tile([P, SP, HEADS], F32)
+        heads_half = N_HALF // SP
+        for half in range(HALVES):
+            proj = psum.tile([P, N_HALF], F32, tag="io%d" % half)
+            for g in range(PASSES):
+                nc.tensor.matmul_mx(
+                    out=proj[:],
+                    lhsT=x_codes[:, g * P : (g + 1) * P].bitcast(FP8X4),
+                    lhsT_scale=x_scales[:, g * P : (g + 1) * P],
+                    rhs=w_words[:, g, 2 * N_HALF * half : 2 * N_HALF * (half + 1)].bitcast(FP4X4),
+                    rhs_scale=w_scales[:, g, N_HALF * half : N_HALF * (half + 1)],
+                    start=(g == 0),
+                    stop=(g == PASSES - 1),
+                )
+            nc.scalar.copy(
+                out=x3_pos[:, :, heads_half * half : heads_half * (half + 1)],
+                in_=proj[:].rearrange("p (h s) -> p s h", s=SP),
+            )
+
+        x3w = keep.tile([P, SIDE, B, WIDE, SP], F32)
+        for k in range(SP // ROWS_PER_BANK):
+            x3_head = psum.tile([P, ROWS_PER_BANK, P], F32, tag="head%d" % k)
+            for q in range(ROWS_PER_BANK):
+                nc.tensor.transpose(x3_head[:, q, :], x3_pos[:, ROWS_PER_BANK * k + q, :], ident[:])
+            s_lo = ROWS_PER_BANK * k
+            for b in range(B):
+                nc.vector.tensor_tensor(
+                    out=x3w[:, :, b, PAD : PAD + SIDE, s_lo : s_lo + ROWS_PER_BANK],
+                    in0=x3_head[:, :, HW * b : HW * (b + 1)].rearrange("p s (i j) -> p i j s", i=SIDE),
+                    in1=bias[:, s_lo : s_lo + ROWS_PER_BANK]
+                    .unsqueeze(1)
+                    .unsqueeze(1)
+                    .to_broadcast([P, SIDE, SIDE, ROWS_PER_BANK]),
+                    op=ALU.add,
+                )
+        last = PAD + SIDE - 1
+        for k in range(1, PAD + 1):
+            nc.vector.tensor_copy(out=x3w[:, :, :, PAD - k, :], in_=x3w[:, :, :, PAD + k, :])
+            nc.vector.tensor_copy(out=x3w[:, :, :, last + k, :], in_=x3w[:, :, :, last - k, :])
+
+        level = [lg[:, b, 0 : TAPS - 1, :] for b in range(B)]
+        for span in (24, 12, 6, 3):
+            for b in range(B):
+                nxt = keep.tile([P, span, HW], BF16, name="max%d_%d" % (span, b))
+                nc.vector.tensor_tensor(
+                    out=nxt[:], in0=level[b][:, 0:span, :], in1=level[b][:, span : 2 * span, :], op=ALU.max
+                )
+                level[b] = nxt[:]
+        peak = keep.tile([P, B, HW], BF16)
+        for b in range(B):
+            nc.vector.tensor_tensor(out=peak[:, b], in0=level[b][:, 0, :], in1=level[b][:, 1, :], op=ALU.max)
+        for b in range(B):
+            nc.vector.tensor_tensor(out=peak[:, b], in0=peak[:, b], in1=level[b][:, 2, :], op=ALU.max)
+        for b in range(B):
+            nc.vector.tensor_tensor(out=peak[:, b], in0=peak[:, b], in1=lg[:, b, TAPS - 1, :], op=ALU.max)
+
+        e = keep.tile([P, WIN, WIN, SIDE, B, SIDE], F32)
+        den_pos = psum.tile([P, P], F32, tag="den_pos")
+        for dy in range(WIN):
+            shifted = shifted_pool.tile([P, B, WIN, HW], F32)
+            nc.vector.tensor_tensor(
+                out=shifted[:],
+                in0=lg[:, :, WIN * dy : WIN * (dy + 1), :],
+                in1=peak[:].unsqueeze(2).to_broadcast([P, B, WIN, HW]),
+                op=ALU.subtract,
+            )
+            for b in range(B):
+                nc.scalar.activation(
+                    out=e[:, dy, :, :, b, :],
+                    in_=shifted[:, b].rearrange("p l (i j) -> p l i j", i=SIDE),
+                    func=ACT.Exp,
+                )
+            for dx in range(WIN):
+                nc.tensor.matmul(
+                    out=den_pos[:],
+                    lhsT=e[:, dy, dx].rearrange("p i b j -> p (i b j)"),
+                    rhs=ident[:],
+                    is_transpose=True,
+                    start=(dy == 0 and dx == 0),
+                    stop=(dy == WIN - 1 and dx == WIN - 1),
+                )
+        den_pos_sb = keep.tile([P, P], F32)
+        nc.scalar.copy(out=den_pos_sb[:], in_=den_pos[:])
+        den_head = psum.tile([P, P], F32, tag="den_head")
+        nc.tensor.transpose(den_head[:], den_pos_sb[:], ident[:])
+        rden = keep.tile([P, SIDE, B, SIDE], F32)
+        nc.vector.reciprocal(out=rden[:].rearrange("p i b j -> p (i b j)"), in_=den_head[:])
+
+        for dy in range(WIN):
+            lo, hi = valid_rows(dy)
+            for i in list(range(0, lo)) + list(range(hi, SIDE)):
+                onto = reflected_tap(dy, i)
+                nc.vector.tensor_tensor(out=e[:, onto, :, i], in0=e[:, onto, :, i], in1=e[:, dy, :, i], op=ALU.add)
+
+        acc = [psum.tile([P, ROWS_PER_BANK, P], F32, name="acc%d" % k, tag="acc%d" % k) for k in range(2)]
+        for dy in range(WIN):
+            lo, hi = valid_rows(dy)
+            for dx in range(WIN):
+                prod = prod_pool.tile([P, SIDE, B, SIDE, SP], F32)
+                nc.vector.tensor_tensor(
+                    out=prod[:, 0 : hi - lo],
+                    in0=x3w[:, lo + dy - PAD : hi + dy - PAD, :, dx : dx + SIDE, :],
+                    in1=e[:, dy, dx, lo:hi].unsqueeze(4).to_broadcast([P, hi - lo, B, SIDE, SP]),
+                    op=ALU.mult,
+                )
+                first_tap = dy == 0 and dx == 0
+                last_tap = dy == WIN - 1 and dx == WIN - 1
+                for i in range(lo, hi):
+                    k = i // ROWS_PER_BANK
+                    bank_rows = [r for r in range(lo, hi) if r // ROWS_PER_BANK == k]
+                    nc.tensor.matmul(
+                        out=acc[k][:, i % ROWS_PER_BANK, :],
+                        lhsT=prod[:, i - lo].rearrange("p b j s -> p (b j s)"),
+                        rhs=ident[:],
+                        is_transpose=True,
+                        start=(first_tap and i == bank_rows[0]),
+                        stop=(last_tap and i == bank_rows[-1]),
+                    )
+
+        acc_sb = keep.tile([P, SIDE, P], F32)
+        out_sb = keep.tile([P, B, SP, SIDE, SIDE], F32)
+        for k in range(2):
+            rows = slice(ROWS_PER_BANK * k, ROWS_PER_BANK * (k + 1))
+            nc.scalar.copy(out=acc_sb[:, rows, :], in_=acc[k][:])
+            num = psum.tile([P, ROWS_PER_BANK, B, SIDE, SP], F32, tag="io%d" % k)
+            for q in range(ROWS_PER_BANK):
+                nc.tensor.transpose(
+                    num[:, q].rearrange("p b j s -> p (b j s)"), acc_sb[:, ROWS_PER_BANK * k + q, :], ident[:]
+                )
+            for b in range(B):
+                nc.vector.tensor_tensor(
+                    out=out_sb[:, b, :, rows, :],
+                    in0=num[:, :, b].rearrange("p i j s -> p s i j"),
+                    in1=rden[:, rows, b, :].unsqueeze(1).to_broadcast([P, SP, ROWS_PER_BANK, SIDE]),
+                    op=ALU.mult,
+                )
+        for b in range(B):
+            nc.sync.dma_start(
+                out=out[b].rearrange("(h s) i j -> h (s i j)", s=SP),
+                in_=out_sb[:, b].rearrange("p s i j -> p (s i j)"),
+            )

@@ -45,12 +45,16 @@ def reflected_tap(dy, i):
     return source - i + PAD
 
 
+DY_GROUPS = [(k, WIN - 1 - k) for k in range(PAD)] + [(PAD,)]
+DY_ORDER = [dy for group in DY_GROUPS for dy in group]
+
+
 def tile_sam_pb_s_kernel(tc, logits, x, w3c_words, w3c_scales, b3c, out):
     nc = tc.nc
     with ExitStack() as ctx:
         keep = ctx.enter_context(tc.tile_pool(name="keep", bufs=1))
-        shifted_pool = ctx.enter_context(tc.tile_pool(name="shifted", bufs=3))
-        prod_pool = ctx.enter_context(tc.tile_pool(name="prod", bufs=4))
+        shifted_pool = ctx.enter_context(tc.tile_pool(name="shifted", bufs=4))
+        prod_pool = ctx.enter_context(tc.tile_pool(name="prod", bufs=6))
         psum = ctx.enter_context(tc.psum_pool(name="psum", bufs=1))
 
         ident = keep.tile([P, P], F32)
@@ -63,6 +67,12 @@ def tile_sam_pb_s_kernel(tc, logits, x, w3c_words, w3c_scales, b3c, out):
             out=x_raw[:].rearrange("p b g t n -> p b g (t n)"),
             in_=x.rearrange("b (g p t) i j -> p b g (t i j)", g=PASSES, p=P, t=PACK),
         )
+        lg = keep.tile([P, B, TAPS, HW], BF16)
+        for b in range(B):
+            nc.sync.dma_start(
+                out=lg[:, b].rearrange("p l n -> p (l n)"),
+                in_=logits[b].rearrange("h l n -> h (l n)"),
+            )
         w_words = keep.tile([P, PASSES, 2 * COUT], U8, align_bytes=64)
         nc.sync.dma_start(
             out=w_words[:].bitcast(I32),
@@ -75,12 +85,6 @@ def tile_sam_pb_s_kernel(tc, logits, x, w3c_words, w3c_scales, b3c, out):
             )
         bias = keep.tile([P, SP], BF16)
         nc.sync.dma_start(out=bias[:], in_=b3c.rearrange("(h s) -> h s", s=SP))
-        lg = keep.tile([P, B, TAPS, HW], BF16)
-        for b in range(B):
-            nc.sync.dma_start(
-                out=lg[:, b].rearrange("p l n -> p (l n)"),
-                in_=logits[b].rearrange("h l n -> h (l n)"),
-            )
 
         grouped = keep.tile([P, PASSES, B, HW, PACK], BF16, align_bytes=64)
         for g in range(PASSES):
@@ -92,6 +96,23 @@ def tile_sam_pb_s_kernel(tc, logits, x, w3c_words, w3c_scales, b3c, out):
             scales=x_scales[:],
             in_=grouped[:].rearrange("p g b n t -> p (g b n t)"),
         )
+
+        level = [lg[:, b, 0 : TAPS - 1, :] for b in range(B)]
+        for span in (24, 12, 6, 3):
+            for b in range(B):
+                nxt = keep.tile([P, span, HW], BF16, name="max%d_%d" % (span, b))
+                nc.vector.tensor_tensor(
+                    out=nxt[:], in0=level[b][:, 0:span, :], in1=level[b][:, span : 2 * span, :], op=ALU.max
+                )
+                level[b] = nxt[:]
+        peak = keep.tile([P, B, HW], BF16)
+        for b in range(B):
+            nc.vector.tensor_tensor(out=peak[:, b], in0=level[b][:, 0, :], in1=level[b][:, 1, :], op=ALU.max)
+        for b in range(B):
+            nc.vector.tensor_tensor(out=peak[:, b], in0=peak[:, b], in1=level[b][:, 2, :], op=ALU.max)
+        for b in range(B):
+            nc.vector.tensor_tensor(out=peak[:, b], in0=peak[:, b], in1=lg[:, b, TAPS - 1, :], op=ALU.max)
+
         x3_pos = keep.tile([P, SP, HEADS], F32)
         heads_half = N_HALF // SP
         for half in range(HALVES):
@@ -111,46 +132,12 @@ def tile_sam_pb_s_kernel(tc, logits, x, w3c_words, w3c_scales, b3c, out):
                 in_=proj[:].rearrange("p (h s) -> p s h", s=SP),
             )
 
-        x3w = keep.tile([P, SIDE, B, WIDE, SP], F32)
-        for k in range(SP // ROWS_PER_BANK):
-            x3_head = psum.tile([P, ROWS_PER_BANK, P], F32, tag="head%d" % k)
-            for q in range(ROWS_PER_BANK):
-                nc.tensor.transpose(x3_head[:, q, :], x3_pos[:, ROWS_PER_BANK * k + q, :], ident[:])
-            s_lo = ROWS_PER_BANK * k
-            for b in range(B):
-                nc.vector.tensor_tensor(
-                    out=x3w[:, :, b, PAD : PAD + SIDE, s_lo : s_lo + ROWS_PER_BANK],
-                    in0=x3_head[:, :, HW * b : HW * (b + 1)].rearrange("p s (i j) -> p i j s", i=SIDE),
-                    in1=bias[:, s_lo : s_lo + ROWS_PER_BANK]
-                    .unsqueeze(1)
-                    .unsqueeze(1)
-                    .to_broadcast([P, SIDE, SIDE, ROWS_PER_BANK]),
-                    op=ALU.add,
-                )
-        last = PAD + SIDE - 1
-        for k in range(1, PAD + 1):
-            nc.vector.tensor_copy(out=x3w[:, :, :, PAD - k, :], in_=x3w[:, :, :, PAD + k, :])
-            nc.vector.tensor_copy(out=x3w[:, :, :, last + k, :], in_=x3w[:, :, :, last - k, :])
-
-        level = [lg[:, b, 0 : TAPS - 1, :] for b in range(B)]
-        for span in (24, 12, 6, 3):
-            for b in range(B):
-                nxt = keep.tile([P, span, HW], BF16, name="max%d_%d" % (span, b))
-                nc.vector.tensor_tensor(
-                    out=nxt[:], in0=level[b][:, 0:span, :], in1=level[b][:, span : 2 * span, :], op=ALU.max
-                )
-                level[b] = nxt[:]
-        peak = keep.tile([P, B, HW], BF16)
-        for b in range(B):
-            nc.vector.tensor_tensor(out=peak[:, b], in0=level[b][:, 0, :], in1=level[b][:, 1, :], op=ALU.max)
-        for b in range(B):
-            nc.vector.tensor_tensor(out=peak[:, b], in0=peak[:, b], in1=level[b][:, 2, :], op=ALU.max)
-        for b in range(B):
-            nc.vector.tensor_tensor(out=peak[:, b], in0=peak[:, b], in1=lg[:, b, TAPS - 1, :], op=ALU.max)
-
         e = keep.tile([P, WIN, WIN, SIDE, B, SIDE], F32)
         den_pos = psum.tile([P, P], F32, tag="den_pos")
-        for dy in range(WIN):
+        x3w = keep.tile([P, SIDE, B, WIDE, SP], F32)
+        acc = [psum.tile([P, ROWS_PER_BANK, P], F32, name="acc%d" % k, tag="acc%d" % k) for k in range(2)]
+
+        def numerators(dy):
             shifted = shifted_pool.tile([P, B, WIN, HW], F32)
             nc.vector.tensor_tensor(
                 out=shifted[:],
@@ -170,24 +157,41 @@ def tile_sam_pb_s_kernel(tc, logits, x, w3c_words, w3c_scales, b3c, out):
                     lhsT=e[:, dy, dx].rearrange("p i b j -> p (i b j)"),
                     rhs=ident[:],
                     is_transpose=True,
-                    start=(dy == 0 and dx == 0),
-                    stop=(dy == WIN - 1 and dx == WIN - 1),
+                    start=(dy == DY_ORDER[0] and dx == 0),
+                    stop=(dy == DY_ORDER[-1] and dx == WIN - 1),
                 )
-        den_pos_sb = keep.tile([P, P], F32)
-        nc.scalar.copy(out=den_pos_sb[:], in_=den_pos[:])
-        den_head = psum.tile([P, P], F32, tag="den_head")
-        nc.tensor.transpose(den_head[:], den_pos_sb[:], ident[:])
-        rden = keep.tile([P, SIDE, B, SIDE], F32)
-        nc.vector.reciprocal(out=rden[:].rearrange("p i b j -> p (i b j)"), in_=den_head[:])
 
-        for dy in range(WIN):
-            lo, hi = valid_rows(dy)
-            for i in list(range(0, lo)) + list(range(hi, SIDE)):
-                onto = reflected_tap(dy, i)
-                nc.vector.tensor_tensor(out=e[:, onto, :, i], in0=e[:, onto, :, i], in1=e[:, dy, :, i], op=ALU.add)
+        def heads_onto_partitions():
+            for k in range(SP // ROWS_PER_BANK):
+                x3_head = psum.tile([P, ROWS_PER_BANK, P], F32, tag="head%d" % k)
+                for q in range(ROWS_PER_BANK):
+                    nc.tensor.transpose(x3_head[:, q, :], x3_pos[:, ROWS_PER_BANK * k + q, :], ident[:])
+                s_lo = ROWS_PER_BANK * k
+                for b in range(B):
+                    nc.vector.tensor_tensor(
+                        out=x3w[:, :, b, PAD : PAD + SIDE, s_lo : s_lo + ROWS_PER_BANK],
+                        in0=x3_head[:, :, HW * b : HW * (b + 1)].rearrange("p s (i j) -> p i j s", i=SIDE),
+                        in1=bias[:, s_lo : s_lo + ROWS_PER_BANK]
+                        .unsqueeze(1)
+                        .unsqueeze(1)
+                        .to_broadcast([P, SIDE, SIDE, ROWS_PER_BANK]),
+                        op=ALU.add,
+                    )
+            last = PAD + SIDE - 1
+            for k in range(1, PAD + 1):
+                nc.vector.tensor_copy(out=x3w[:, :, :, PAD - k, :], in_=x3w[:, :, :, PAD + k, :])
+                nc.vector.tensor_copy(out=x3w[:, :, :, last + k, :], in_=x3w[:, :, :, last - k, :])
 
-        acc = [psum.tile([P, ROWS_PER_BANK, P], F32, name="acc%d" % k, tag="acc%d" % k) for k in range(2)]
-        for dy in range(WIN):
+        def fold_onto(dy):
+            for other in range(WIN):
+                lo, hi = valid_rows(other)
+                for i in list(range(0, lo)) + list(range(hi, SIDE)):
+                    if reflected_tap(other, i) == dy:
+                        nc.vector.tensor_tensor(
+                            out=e[:, dy, :, i], in0=e[:, dy, :, i], in1=e[:, other, :, i], op=ALU.add
+                        )
+
+        def weigh(dy):
             lo, hi = valid_rows(dy)
             for dx in range(WIN):
                 prod = prod_pool.tile([P, SIDE, B, SIDE, SP], F32)
@@ -197,8 +201,8 @@ def tile_sam_pb_s_kernel(tc, logits, x, w3c_words, w3c_scales, b3c, out):
                     in1=e[:, dy, dx, lo:hi].unsqueeze(4).to_broadcast([P, hi - lo, B, SIDE, SP]),
                     op=ALU.mult,
                 )
-                first_tap = dy == 0 and dx == 0
-                last_tap = dy == WIN - 1 and dx == WIN - 1
+                first_tap = dy == DY_ORDER[0] and dx == 0
+                last_tap = dy == DY_ORDER[-1] and dx == WIN - 1
                 for i in range(lo, hi):
                     k = i // ROWS_PER_BANK
                     bank_rows = [r for r in range(lo, hi) if r // ROWS_PER_BANK == k]
@@ -211,24 +215,49 @@ def tile_sam_pb_s_kernel(tc, logits, x, w3c_words, w3c_scales, b3c, out):
                         stop=(last_tap and i == bank_rows[-1]),
                     )
 
+        def main_loop():
+            for dy in DY_GROUPS[0]:
+                numerators(dy)
+            for n, group in enumerate(DY_GROUPS):
+                for dy in DY_GROUPS[n + 1] if n + 1 < len(DY_GROUPS) else ():
+                    numerators(dy)
+                if n == 0:
+                    heads_onto_partitions()
+                for dy in group:
+                    fold_onto(dy)
+                for dy in group:
+                    weigh(dy)
+
+        main_loop()
+
+        den_pos_sb = keep.tile([P, P], F32)
+        nc.scalar.copy(out=den_pos_sb[:], in_=den_pos[:])
+        den_head = psum.tile([P, P], F32, tag="den_head")
+        nc.tensor.transpose(den_head[:], den_pos_sb[:], ident[:])
+        rden = keep.tile([P, SIDE, B, SIDE], F32)
+        nc.vector.reciprocal(out=rden[:].rearrange("p i b j -> p (i b j)"), in_=den_head[:])
+
         acc_sb = keep.tile([P, SIDE, P], F32)
         out_sb = keep.tile([P, B, SP, SIDE, SIDE], F32)
+        num = []
+        nc.scalar.copy(out=acc_sb[:, 0:ROWS_PER_BANK, :], in_=acc[0][:])
+        nc.vector.tensor_copy(out=acc_sb[:, ROWS_PER_BANK:SIDE, :], in_=acc[1][:])
         for k in range(2):
-            rows = slice(ROWS_PER_BANK * k, ROWS_PER_BANK * (k + 1))
-            nc.scalar.copy(out=acc_sb[:, rows, :], in_=acc[k][:])
-            num = psum.tile([P, ROWS_PER_BANK, B, SIDE, SP], F32, tag="io%d" % k)
+            num_k = psum.tile([P, ROWS_PER_BANK, B, SIDE, SP], F32, name="num%d" % k, tag="io%d" % k)
             for q in range(ROWS_PER_BANK):
                 nc.tensor.transpose(
-                    num[:, q].rearrange("p b j s -> p (b j s)"), acc_sb[:, ROWS_PER_BANK * k + q, :], ident[:]
+                    num_k[:, q].rearrange("p b j s -> p (b j s)"), acc_sb[:, ROWS_PER_BANK * k + q, :], ident[:]
                 )
-            for b in range(B):
+            num.append(num_k)
+        for b in range(B):
+            for k in range(2):
+                rows = slice(ROWS_PER_BANK * k, ROWS_PER_BANK * (k + 1))
                 nc.vector.tensor_tensor(
                     out=out_sb[:, b, :, rows, :],
-                    in0=num[:, :, b].rearrange("p i j s -> p s i j"),
+                    in0=num[k][:, :, b].rearrange("p i j s -> p s i j"),
                     in1=rden[:, rows, b, :].unsqueeze(1).to_broadcast([P, SP, ROWS_PER_BANK, SIDE]),
                     op=ALU.mult,
                 )
-        for b in range(B):
             nc.sync.dma_start(
                 out=out[b].rearrange("(h s) i j -> h (s i j)", s=SP),
                 in_=out_sb[:, b].rearrange("p s i j -> p (s i j)"),

@@ -30,13 +30,14 @@ K_PASS = P * PACK
 PASSES = CIN // K_PASS
 N_HALF = 512
 HALVES = COUT // N_HALF
-ROWS_PER_BANK = 4
+PER_BANK = 4
+DX_PITCH = 8
 
 FLOPS = 2 * B * HW * CIN * COUT + 2 * B * COUT * HW * TAPS
 
 
-def valid_rows(dy):
-    return max(0, PAD - dy), min(SIDE, SIDE + PAD - dy)
+def valid_taps(i):
+    return max(0, PAD - i), min(WIN, SIDE + PAD - i)
 
 
 def reflected_tap(dy, i):
@@ -45,17 +46,15 @@ def reflected_tap(dy, i):
     return source - i + PAD
 
 
-DY_GROUPS = [(k, WIN - 1 - k) for k in range(PAD)] + [(PAD,)]
-DY_ORDER = [dy for group in DY_GROUPS for dy in group]
-
-
 def tile_sam_pb_s_kernel(tc, logits, x, w3c_words, w3c_scales, b3c, out):
     nc = tc.nc
     with ExitStack() as ctx:
         keep = ctx.enter_context(tc.tile_pool(name="keep", bufs=1))
-        shifted_pool = ctx.enter_context(tc.tile_pool(name="shifted", bufs=4))
         prod_pool = ctx.enter_context(tc.tile_pool(name="prod", bufs=6))
+        row_pool = ctx.enter_context(tc.tile_pool(name="row", bufs=2))
         psum = ctx.enter_context(tc.psum_pool(name="psum", bufs=1))
+        acc_pool = ctx.enter_context(tc.psum_pool(name="acc", bufs=2))
+        num_pool = ctx.enter_context(tc.psum_pool(name="num", bufs=2))
 
         ident = keep.tile([P, P], F32)
         make_identity(nc, ident[:])
@@ -67,10 +66,10 @@ def tile_sam_pb_s_kernel(tc, logits, x, w3c_words, w3c_scales, b3c, out):
             out=x_raw[:].rearrange("p b g t n -> p b g (t n)"),
             in_=x.rearrange("b (g p t) i j -> p b g (t i j)", g=PASSES, p=P, t=PACK),
         )
-        lg = keep.tile([P, B, TAPS, HW], BF16)
+        lg = keep.tile([P, B, WIN, WIN, SIDE, SIDE], BF16)
         for b in range(B):
             nc.sync.dma_start(
-                out=lg[:, b].rearrange("p l n -> p (l n)"),
+                out=lg[:, b].rearrange("p u v i j -> p (u v i j)"),
                 in_=logits[b].rearrange("h l n -> h (l n)"),
             )
         w_words = keep.tile([P, PASSES, 2 * COUT], U8, align_bytes=64)
@@ -97,7 +96,8 @@ def tile_sam_pb_s_kernel(tc, logits, x, w3c_words, w3c_scales, b3c, out):
             in_=grouped[:].rearrange("p g b n t -> p (g b n t)"),
         )
 
-        level = [lg[:, b, 0 : TAPS - 1, :] for b in range(B)]
+        taps = [lg[:, b].rearrange("p u v i j -> p (u v) (i j)") for b in range(B)]
+        level = [taps[b][:, 0 : TAPS - 1, :] for b in range(B)]
         for span in (24, 12, 6, 3):
             for b in range(B):
                 nxt = keep.tile([P, span, HW], BF16, name="max%d_%d" % (span, b))
@@ -106,17 +106,22 @@ def tile_sam_pb_s_kernel(tc, logits, x, w3c_words, w3c_scales, b3c, out):
                 )
                 level[b] = nxt[:]
         peak = keep.tile([P, B, HW], BF16)
+        neg_peak = keep.tile([P, B, SIDE, SIDE], F32)
         for b in range(B):
             nc.vector.tensor_tensor(out=peak[:, b], in0=level[b][:, 0, :], in1=level[b][:, 1, :], op=ALU.max)
         for b in range(B):
             nc.vector.tensor_tensor(out=peak[:, b], in0=peak[:, b], in1=level[b][:, 2, :], op=ALU.max)
         for b in range(B):
-            nc.vector.tensor_tensor(out=peak[:, b], in0=peak[:, b], in1=lg[:, b, TAPS - 1, :], op=ALU.max)
+            nc.vector.tensor_tensor(out=peak[:, b], in0=peak[:, b], in1=taps[b][:, TAPS - 1, :], op=ALU.max)
+        for b in range(B):
+            nc.vector.tensor_scalar_mul(
+                out=neg_peak[:, b].rearrange("p i j -> p (i j)"), in0=peak[:, b], scalar1=-1.0
+            )
 
         x3_pos = keep.tile([P, SP, HEADS], F32)
         heads_half = N_HALF // SP
         for half in range(HALVES):
-            proj = psum.tile([P, N_HALF], F32, tag="io%d" % half)
+            proj = psum.tile([P, N_HALF], F32, tag="proj%d" % half)
             for g in range(PASSES):
                 nc.tensor.matmul_mx(
                     out=proj[:],
@@ -127,137 +132,105 @@ def tile_sam_pb_s_kernel(tc, logits, x, w3c_words, w3c_scales, b3c, out):
                     start=(g == 0),
                     stop=(g == PASSES - 1),
                 )
-            nc.scalar.copy(
+            nc.vector.tensor_copy(
                 out=x3_pos[:, :, heads_half * half : heads_half * (half + 1)],
                 in_=proj[:].rearrange("p (h s) -> p s h", s=SP),
             )
 
-        e = keep.tile([P, WIN, WIN, SIDE, B, SIDE], F32)
-        den_pos = psum.tile([P, P], F32, tag="den_pos")
         x3w = keep.tile([P, SIDE, B, WIDE, SP], F32)
-        acc = [psum.tile([P, ROWS_PER_BANK, P], F32, name="acc%d" % k, tag="acc%d" % k) for k in range(2)]
-
-        def numerators(dy):
-            shifted = shifted_pool.tile([P, B, WIN, HW], F32)
-            nc.vector.tensor_tensor(
-                out=shifted[:],
-                in0=lg[:, :, WIN * dy : WIN * (dy + 1), :],
-                in1=peak[:].unsqueeze(2).to_broadcast([P, B, WIN, HW]),
-                op=ALU.subtract,
-            )
+        for k in range(SP // PER_BANK):
+            x3_head = psum.tile([P, PER_BANK, P], F32, tag="head%d" % k)
+            for q in range(PER_BANK):
+                nc.tensor.transpose(x3_head[:, q, :], x3_pos[:, PER_BANK * k + q, :], ident[:])
+            s_lo = PER_BANK * k
             for b in range(B):
-                nc.scalar.activation(
-                    out=e[:, dy, :, :, b, :],
-                    in_=shifted[:, b].rearrange("p l (i j) -> p l i j", i=SIDE),
-                    func=ACT.Exp,
+                nc.vector.tensor_tensor(
+                    out=x3w[:, :, b, PAD : PAD + SIDE, s_lo : s_lo + PER_BANK],
+                    in0=x3_head[:, :, HW * b : HW * (b + 1)].rearrange("p s (i j) -> p i j s", i=SIDE),
+                    in1=bias[:, s_lo : s_lo + PER_BANK].unsqueeze(1).unsqueeze(1).to_broadcast([P, SIDE, SIDE, PER_BANK]),
+                    op=ALU.add,
                 )
-            for dx in range(WIN):
-                nc.tensor.matmul(
-                    out=den_pos[:],
-                    lhsT=e[:, dy, dx].rearrange("p i b j -> p (i b j)"),
-                    rhs=ident[:],
-                    is_transpose=True,
-                    start=(dy == DY_ORDER[0] and dx == 0),
-                    stop=(dy == DY_ORDER[-1] and dx == WIN - 1),
-                )
+        last = PAD + SIDE - 1
+        for k in range(1, PAD + 1):
+            nc.vector.tensor_copy(out=x3w[:, :, :, PAD - k, :], in_=x3w[:, :, :, PAD + k, :])
+            nc.vector.tensor_copy(out=x3w[:, :, :, last + k, :], in_=x3w[:, :, :, last - k, :])
 
-        def heads_onto_partitions():
-            for k in range(SP // ROWS_PER_BANK):
-                x3_head = psum.tile([P, ROWS_PER_BANK, P], F32, tag="head%d" % k)
-                for q in range(ROWS_PER_BANK):
-                    nc.tensor.transpose(x3_head[:, q, :], x3_pos[:, ROWS_PER_BANK * k + q, :], ident[:])
-                s_lo = ROWS_PER_BANK * k
-                for b in range(B):
-                    nc.vector.tensor_tensor(
-                        out=x3w[:, :, b, PAD : PAD + SIDE, s_lo : s_lo + ROWS_PER_BANK],
-                        in0=x3_head[:, :, HW * b : HW * (b + 1)].rearrange("p s (i j) -> p i j s", i=SIDE),
-                        in1=bias[:, s_lo : s_lo + ROWS_PER_BANK]
-                        .unsqueeze(1)
-                        .unsqueeze(1)
-                        .to_broadcast([P, SIDE, SIDE, ROWS_PER_BANK]),
-                        op=ALU.add,
+        e = keep.tile([P, SIDE, B, SIDE, WIN, DX_PITCH], F32)
+        den = keep.tile([P, SIDE, B, SIDE], F32)
+        rden = keep.tile([P, SIDE, B, SIDE], F32)
+        out_sb = keep.tile([P, B, SP, SIDE, SIDE], F32)
+        acc = {}
+
+        def numerators(i):
+            for b in range(B):
+                for j in range(SIDE):
+                    nc.scalar.activation(
+                        out=e[:, i, b, j, :, 0:WIN],
+                        in_=lg[:, b, :, :, i, j],
+                        func=ACT.Exp,
+                        bias=neg_peak[:, b, i, j : j + 1],
+                        accum_out=den[:, i, b, j : j + 1],
                     )
-            last = PAD + SIDE - 1
-            for k in range(1, PAD + 1):
-                nc.vector.tensor_copy(out=x3w[:, :, :, PAD - k, :], in_=x3w[:, :, :, PAD + k, :])
-                nc.vector.tensor_copy(out=x3w[:, :, :, last + k, :], in_=x3w[:, :, :, last - k, :])
 
-        def fold_onto(dy):
-            for other in range(WIN):
-                lo, hi = valid_rows(other)
-                for i in list(range(0, lo)) + list(range(hi, SIDE)):
-                    if reflected_tap(other, i) == dy:
-                        nc.vector.tensor_tensor(
-                            out=e[:, dy, :, i], in0=e[:, dy, :, i], in1=e[:, other, :, i], op=ALU.add
-                        )
+        def fold(i):
+            lo, hi = valid_taps(i)
+            for dy in list(range(0, lo)) + list(range(hi, WIN)):
+                onto = reflected_tap(dy, i)
+                nc.vector.tensor_tensor(
+                    out=e[:, i, :, :, onto, 0:WIN], in0=e[:, i, :, :, onto, 0:WIN], in1=e[:, i, :, :, dy, 0:WIN], op=ALU.add
+                )
 
-        def weigh(dy):
-            lo, hi = valid_rows(dy)
+        def weigh(i):
+            lo, hi = valid_taps(i)
+            acc[i] = acc_pool.tile([P, P], F32, name="acc")
             for dx in range(WIN):
-                prod = prod_pool.tile([P, SIDE, B, SIDE, SP], F32)
+                prod = prod_pool.tile([P, WIN, B, SIDE, SP], F32)
                 nc.vector.tensor_tensor(
                     out=prod[:, 0 : hi - lo],
-                    in0=x3w[:, lo + dy - PAD : hi + dy - PAD, :, dx : dx + SIDE, :],
-                    in1=e[:, dy, dx, lo:hi].unsqueeze(4).to_broadcast([P, hi - lo, B, SIDE, SP]),
+                    in0=x3w[:, i + lo - PAD : i + hi - PAD, :, dx : dx + SIDE, :],
+                    in1=e[:, i, :, :, lo:hi, dx]
+                    .rearrange("p b j d -> p d b j")
+                    .unsqueeze(4)
+                    .to_broadcast([P, hi - lo, B, SIDE, SP]),
                     op=ALU.mult,
                 )
-                first_tap = dy == DY_ORDER[0] and dx == 0
-                last_tap = dy == DY_ORDER[-1] and dx == WIN - 1
-                for i in range(lo, hi):
-                    k = i // ROWS_PER_BANK
-                    bank_rows = [r for r in range(lo, hi) if r // ROWS_PER_BANK == k]
+                for dy in range(lo, hi):
                     nc.tensor.matmul(
-                        out=acc[k][:, i % ROWS_PER_BANK, :],
-                        lhsT=prod[:, i - lo].rearrange("p b j s -> p (b j s)"),
+                        out=acc[i][:],
+                        lhsT=prod[:, dy - lo].rearrange("p b j s -> p (b j s)"),
                         rhs=ident[:],
                         is_transpose=True,
-                        start=(first_tap and i == bank_rows[0]),
-                        stop=(last_tap and i == bank_rows[-1]),
+                        start=(dx == 0 and dy == lo),
+                        stop=(dx == WIN - 1 and dy == hi - 1),
                     )
 
-        def main_loop():
-            for dy in DY_GROUPS[0]:
-                numerators(dy)
-            for n, group in enumerate(DY_GROUPS):
-                for dy in DY_GROUPS[n + 1] if n + 1 < len(DY_GROUPS) else ():
-                    numerators(dy)
-                if n == 0:
-                    heads_onto_partitions()
-                for dy in group:
-                    fold_onto(dy)
-                for dy in group:
-                    weigh(dy)
+        def finish(i):
+            acc_sb = row_pool.tile([P, P], F32)
+            nc.scalar.copy(out=acc_sb[:], in_=acc[i][:])
+            num = num_pool.tile([P, B, SIDE, SP], F32)
+            nc.tensor.transpose(num[:].rearrange("p b j s -> p (b j s)"), acc_sb[:], ident[:])
+            nc.vector.reciprocal(out=rden[:, i], in_=den[:, i])
+            nc.vector.tensor_tensor(
+                out=out_sb[:, :, :, i, :],
+                in0=num[:].rearrange("p b j s -> p b s j"),
+                in1=rden[:, i].unsqueeze(2).to_broadcast([P, B, SP, SIDE]),
+                op=ALU.mult,
+            )
 
-        main_loop()
+        def rows():
+            numerators(0)
+            for i in range(SIDE):
+                if i + 1 < SIDE:
+                    numerators(i + 1)
+                fold(i)
+                weigh(i)
+                if i > 0:
+                    finish(i - 1)
+            finish(SIDE - 1)
 
-        den_pos_sb = keep.tile([P, P], F32)
-        nc.scalar.copy(out=den_pos_sb[:], in_=den_pos[:])
-        den_head = psum.tile([P, P], F32, tag="den_head")
-        nc.tensor.transpose(den_head[:], den_pos_sb[:], ident[:])
-        rden = keep.tile([P, SIDE, B, SIDE], F32)
-        nc.vector.reciprocal(out=rden[:].rearrange("p i b j -> p (i b j)"), in_=den_head[:])
+        rows()
 
-        acc_sb = keep.tile([P, SIDE, P], F32)
-        out_sb = keep.tile([P, B, SP, SIDE, SIDE], F32)
-        num = []
-        nc.scalar.copy(out=acc_sb[:, 0:ROWS_PER_BANK, :], in_=acc[0][:])
-        nc.vector.tensor_copy(out=acc_sb[:, ROWS_PER_BANK:SIDE, :], in_=acc[1][:])
-        for k in range(2):
-            num_k = psum.tile([P, ROWS_PER_BANK, B, SIDE, SP], F32, name="num%d" % k, tag="io%d" % k)
-            for q in range(ROWS_PER_BANK):
-                nc.tensor.transpose(
-                    num_k[:, q].rearrange("p b j s -> p (b j s)"), acc_sb[:, ROWS_PER_BANK * k + q, :], ident[:]
-                )
-            num.append(num_k)
         for b in range(B):
-            for k in range(2):
-                rows = slice(ROWS_PER_BANK * k, ROWS_PER_BANK * (k + 1))
-                nc.vector.tensor_tensor(
-                    out=out_sb[:, b, :, rows, :],
-                    in0=num[k][:, :, b].rearrange("p i j s -> p s i j"),
-                    in1=rden[:, rows, b, :].unsqueeze(1).to_broadcast([P, SP, ROWS_PER_BANK, SIDE]),
-                    op=ALU.mult,
-                )
             nc.sync.dma_start(
                 out=out[b].rearrange("(h s) i j -> h (s i j)", s=SP),
                 in_=out_sb[:, b].rearrange("p s i j -> p (s i j)"),

@@ -31,7 +31,9 @@ PASSES = CIN // K_PASS
 N_HALF = 512
 HALVES = COUT // N_HALF
 PER_BANK = 4
-DX_PITCH = 8
+E_PITCH = WIDE + 1
+E_BLOCK = SIDE * E_PITCH
+PROD_SETS = 2
 
 FLOPS = 2 * B * HW * CIN * COUT + 2 * B * COUT * HW * TAPS
 
@@ -46,11 +48,14 @@ def reflected_tap(dy, i):
     return source - i + PAD
 
 
+def valid_positions(dx):
+    return max(0, PAD - dx), min(SIDE, SIDE + PAD - dx)
+
+
 def tile_sam_pb_s_kernel(tc, logits, x, w3c_words, w3c_scales, b3c, out):
     nc = tc.nc
     with ExitStack() as ctx:
         keep = ctx.enter_context(tc.tile_pool(name="keep", bufs=1))
-        prod_pool = ctx.enter_context(tc.tile_pool(name="prod", bufs=6))
         row_pool = ctx.enter_context(tc.tile_pool(name="row", bufs=2))
         psum = ctx.enter_context(tc.psum_pool(name="psum", bufs=1))
         acc_pool = ctx.enter_context(tc.psum_pool(name="acc", bufs=2))
@@ -60,6 +65,23 @@ def tile_sam_pb_s_kernel(tc, logits, x, w3c_words, w3c_scales, b3c, out):
         make_identity(nc, ident[:])
         w_scales = keep.tile([P, PASSES, COUT], U8, align_bytes=64)
         nc.vector.memset(w_scales[:].bitcast(I32), 0)
+
+        e = keep.tile([P, SIDE, WIN, B, E_BLOCK], F32)
+        e_cells = e[:].rearrange("p i d b (j c) -> p (i d b) j c", c=E_PITCH)
+        nc.vector.memset(e_cells[:, :, 0:2, E_PITCH - 2 : E_PITCH], 0.0)
+        nc.vector.memset(e_cells[:, :, SIDE - 3 : SIDE - 1, WIN : WIN + 2], 0.0)
+        prods = []
+        for dx in range(WIN):
+            j_lo, j_hi = valid_positions(dx)
+            sets = []
+            for k in range(PROD_SETS):
+                prod = keep.tile([P, WIN, B, SIDE, SP], F32, name="prod%d_%d" % (dx, k))
+                if j_lo > 0:
+                    nc.gpsimd.memset(prod[:, :, :, 0:j_lo, :], 0.0)
+                if j_hi < SIDE:
+                    nc.gpsimd.memset(prod[:, :, :, j_hi:SIDE, :], 0.0)
+                sets.append(prod)
+            prods.append(sets)
 
         x_raw = keep.tile([P, B, PASSES, PACK, HW], BF16)
         nc.sync.dma_start(
@@ -137,7 +159,7 @@ def tile_sam_pb_s_kernel(tc, logits, x, w3c_words, w3c_scales, b3c, out):
                 in_=proj[:].rearrange("p (h s) -> p s h", s=SP),
             )
 
-        x3w = keep.tile([P, SIDE, B, WIDE, SP], F32)
+        x3w = keep.tile([P, SIDE, B, SIDE, SP], F32)
         for k in range(SP // PER_BANK):
             x3_head = psum.tile([P, PER_BANK, P], F32, tag="head%d" % k)
             for q in range(PER_BANK):
@@ -145,17 +167,12 @@ def tile_sam_pb_s_kernel(tc, logits, x, w3c_words, w3c_scales, b3c, out):
             s_lo = PER_BANK * k
             for b in range(B):
                 nc.vector.tensor_tensor(
-                    out=x3w[:, :, b, PAD : PAD + SIDE, s_lo : s_lo + PER_BANK],
+                    out=x3w[:, :, b, :, s_lo : s_lo + PER_BANK],
                     in0=x3_head[:, :, HW * b : HW * (b + 1)].rearrange("p s (i j) -> p i j s", i=SIDE),
                     in1=bias[:, s_lo : s_lo + PER_BANK].unsqueeze(1).unsqueeze(1).to_broadcast([P, SIDE, SIDE, PER_BANK]),
                     op=ALU.add,
                 )
-        last = PAD + SIDE - 1
-        for k in range(1, PAD + 1):
-            nc.vector.tensor_copy(out=x3w[:, :, :, PAD - k, :], in_=x3w[:, :, :, PAD + k, :])
-            nc.vector.tensor_copy(out=x3w[:, :, :, last + k, :], in_=x3w[:, :, :, last - k, :])
 
-        e = keep.tile([P, SIDE, B, SIDE, WIN, DX_PITCH], F32)
         den = keep.tile([P, SIDE, B, SIDE], F32)
         rden = keep.tile([P, SIDE, B, SIDE], F32)
         out_sb = keep.tile([P, B, SP, SIDE, SIDE], F32)
@@ -165,7 +182,7 @@ def tile_sam_pb_s_kernel(tc, logits, x, w3c_words, w3c_scales, b3c, out):
             for b in range(B):
                 for j in range(SIDE):
                     nc.scalar.activation(
-                        out=e[:, i, b, j, :, 0:WIN],
+                        out=e[:, i, :, b, E_PITCH * j : E_PITCH * j + WIN],
                         in_=lg[:, b, :, :, i, j],
                         func=ACT.Exp,
                         bias=neg_peak[:, b, i, j : j + 1],
@@ -174,24 +191,50 @@ def tile_sam_pb_s_kernel(tc, logits, x, w3c_words, w3c_scales, b3c, out):
 
         def fold(i):
             lo, hi = valid_taps(i)
-            for dy in list(range(0, lo)) + list(range(hi, WIN)):
-                onto = reflected_tap(dy, i)
+            by_tap = e[:, i].rearrange("p d b (j c) -> p d b j c", c=E_PITCH)
+            if lo > 0:
+                onto = reflected_tap(lo - 1, i)
                 nc.vector.tensor_tensor(
-                    out=e[:, i, :, :, onto, 0:WIN], in0=e[:, i, :, :, onto, 0:WIN], in1=e[:, i, :, :, dy, 0:WIN], op=ALU.add
+                    out=by_tap[:, onto : onto + lo, :, :, 0:WIN],
+                    in0=by_tap[:, onto : onto + lo, :, :, 0:WIN],
+                    in1=by_tap[:, lo - 1 :: -1, :, :, 0:WIN],
+                    op=ALU.add,
                 )
+            if hi < WIN:
+                onto = reflected_tap(WIN - 1, i)
+                nc.vector.tensor_tensor(
+                    out=by_tap[:, onto : onto + WIN - hi, :, :, 0:WIN],
+                    in0=by_tap[:, onto : onto + WIN - hi, :, :, 0:WIN],
+                    in1=by_tap[:, WIN - 1 : hi - 1 : -1, :, :, 0:WIN],
+                    op=ALU.add,
+                )
+            by_col = e[:, i, :, :, 0 : SIDE * WIDE].rearrange("p d b (j c) -> p d b j c", c=WIDE)
+            nc.vector.tensor_tensor(
+                out=by_col[:, lo:hi, :, 0:PAD, PAD + 1 : 2 * PAD + 1],
+                in0=by_col[:, lo:hi, :, 0:PAD, PAD + 1 : 2 * PAD + 1],
+                in1=by_col[:, lo:hi, :, 0:PAD, PAD - 1 :: -1],
+                op=ALU.add,
+            )
+            nc.vector.tensor_tensor(
+                out=by_col[:, lo:hi, :, SIDE - PAD : SIDE, SIDE - 1 : SIDE + PAD - 1],
+                in0=by_col[:, lo:hi, :, SIDE - PAD : SIDE, SIDE - 1 : SIDE + PAD - 1],
+                in1=by_col[:, lo:hi, :, SIDE - PAD : SIDE, WIDE - 1 : WIDE - PAD - 1 : -1],
+                op=ALU.add,
+            )
 
         def weigh(i):
             lo, hi = valid_taps(i)
+            by_tap = e[:, i].rearrange("p d b (j c) -> p d b j c", c=E_PITCH)
             acc[i] = acc_pool.tile([P, P], F32, name="acc")
             for dx in range(WIN):
-                prod = prod_pool.tile([P, WIN, B, SIDE, SP], F32)
+                j_lo, j_hi = valid_positions(dx)
+                prod = prods[dx][i % PROD_SETS]
                 nc.vector.tensor_tensor(
-                    out=prod[:, 0 : hi - lo],
-                    in0=x3w[:, i + lo - PAD : i + hi - PAD, :, dx : dx + SIDE, :],
-                    in1=e[:, i, :, :, lo:hi, dx]
-                    .rearrange("p b j d -> p d b j")
+                    out=prod[:, 0 : hi - lo, :, j_lo:j_hi, :],
+                    in0=x3w[:, i + lo - PAD : i + hi - PAD, :, j_lo + dx - PAD : j_hi + dx - PAD, :],
+                    in1=by_tap[:, lo:hi, :, j_lo:j_hi, dx]
                     .unsqueeze(4)
-                    .to_broadcast([P, hi - lo, B, SIDE, SP]),
+                    .to_broadcast([P, hi - lo, B, j_hi - j_lo, SP]),
                     op=ALU.mult,
                 )
                 for dy in range(lo, hi):

@@ -34,6 +34,7 @@ PER_BANK = 4
 E_PITCH = WIDE + 1
 E_BLOCK = SIDE * E_PITCH
 PROD_SETS = 2
+POOL_COLUMNS = (2, 4)
 
 FLOPS = 2 * B * HW * CIN * COUT + 2 * B * COUT * HW * TAPS
 
@@ -83,6 +84,8 @@ def tile_sam_pb_s_kernel(tc, logits, x, w3c_words, w3c_scales, b3c, out):
                 sets.append(prod)
             prods.append(sets)
 
+        bias_prods = [keep.tile([P, B, SIDE, SP], F32, name="bias_prod%d" % k) for k in range(PROD_SETS)]
+
         x_raw = keep.tile([P, B, PASSES, PACK, HW], BF16)
         nc.sync.dma_start(
             out=x_raw[:].rearrange("p b g t n -> p b g (t n)"),
@@ -107,15 +110,16 @@ def tile_sam_pb_s_kernel(tc, logits, x, w3c_words, w3c_scales, b3c, out):
         bias = keep.tile([P, SP], BF16)
         nc.sync.dma_start(out=bias[:], in_=b3c.rearrange("(h s) -> h s", s=SP))
 
-        grouped = keep.tile([P, PASSES, B, HW, PACK], BF16, align_bytes=64)
+        grouped = keep.tile([P, PASSES, SIDE, B, SIDE, PACK], BF16, align_bytes=64)
         for g in range(PASSES):
-            nc.scalar.copy(out=grouped[:, g], in_=x_raw[:, :, g].rearrange("p b t n -> p b n t"))
+            for b in range(B):
+                nc.scalar.copy(out=grouped[:, g, :, b], in_=x_raw[:, b, g].rearrange("p t (i j) -> p i j t", i=SIDE))
         x_codes = keep.tile([P, PASSES * P], U32, align_bytes=64)
         x_scales = keep.tile([P, PASSES * P], U8, align_bytes=64)
         nc.vector.quantize_mx(
             out=x_codes[:].bitcast(FP8X4),
             scales=x_scales[:],
-            in_=grouped[:].rearrange("p g b n t -> p (g b n t)"),
+            in_=grouped[:].rearrange("p g i b j t -> p (g i b j t)"),
         )
 
         taps = [lg[:, b].rearrange("p u v i j -> p (u v) (i j)") for b in range(B)]
@@ -154,24 +158,19 @@ def tile_sam_pb_s_kernel(tc, logits, x, w3c_words, w3c_scales, b3c, out):
                     start=(g == 0),
                     stop=(g == PASSES - 1),
                 )
-            nc.vector.tensor_copy(
+            nc.scalar.copy(
                 out=x3_pos[:, :, heads_half * half : heads_half * (half + 1)],
                 in_=proj[:].rearrange("p (h s) -> p s h", s=SP),
             )
 
         x3w = keep.tile([P, SIDE, B, SIDE, SP], F32)
+        x3_rows = []
         for k in range(SP // PER_BANK):
             x3_head = psum.tile([P, PER_BANK, P], F32, tag="head%d" % k)
             for q in range(PER_BANK):
                 nc.tensor.transpose(x3_head[:, q, :], x3_pos[:, PER_BANK * k + q, :], ident[:])
-            s_lo = PER_BANK * k
-            for b in range(B):
-                nc.vector.tensor_tensor(
-                    out=x3w[:, :, b, :, s_lo : s_lo + PER_BANK],
-                    in0=x3_head[:, :, HW * b : HW * (b + 1)].rearrange("p s (i j) -> p i j s", i=SIDE),
-                    in1=bias[:, s_lo : s_lo + PER_BANK].unsqueeze(1).unsqueeze(1).to_broadcast([P, SIDE, SIDE, PER_BANK]),
-                    op=ALU.add,
-                )
+            x3_rows.append(x3_head[:].rearrange("p s (i b j) -> p i b j s", b=B, i=SIDE))
+            nc.vector.tensor_copy(out=x3w[:, :, :, :, PER_BANK * k : PER_BANK * (k + 1)], in_=x3_rows[k])
 
         den = keep.tile([P, SIDE, B, SIDE], F32)
         rden = keep.tile([P, SIDE, B, SIDE], F32)
@@ -221,38 +220,67 @@ def tile_sam_pb_s_kernel(tc, logits, x, w3c_words, w3c_scales, b3c, out):
                 in1=by_col[:, lo:hi, :, SIDE - PAD : SIDE, WIDE - 1 : WIDE - PAD - 1 : -1],
                 op=ALU.add,
             )
+            nc.vector.tensor_tensor(
+                out=bias_prods[i % PROD_SETS][:],
+                in0=den[:, i].unsqueeze(3).to_broadcast([P, B, SIDE, SP]),
+                in1=bias[:].unsqueeze(1).unsqueeze(1).to_broadcast([P, B, SIDE, SP]),
+                op=ALU.mult,
+            )
+            nc.vector.reciprocal(out=rden[:, i], in_=den[:, i])
 
         def weigh(i):
             lo, hi = valid_taps(i)
+            rows_in = slice(i + lo - PAD, i + hi - PAD)
             by_tap = e[:, i].rearrange("p d b (j c) -> p d b j c", c=E_PITCH)
             acc[i] = acc_pool.tile([P, P], F32, name="acc")
-            for dx in range(WIN):
+            left = [1 + WIN * (hi - lo)]
+
+            def add_up(block):
+                nc.tensor.matmul(
+                    out=acc[i][:],
+                    lhsT=block.rearrange("p b j s -> p (b j s)"),
+                    rhs=ident[:],
+                    is_transpose=True,
+                    start=(left[0] == 1 + WIN * (hi - lo)),
+                    stop=(left[0] == 1),
+                )
+                left[0] -= 1
+
+            def weights(dx, width):
                 j_lo, j_hi = valid_positions(dx)
-                prod = prods[dx][i % PROD_SETS]
-                nc.vector.tensor_tensor(
-                    out=prod[:, 0 : hi - lo, :, j_lo:j_hi, :],
-                    in0=x3w[:, i + lo - PAD : i + hi - PAD, :, j_lo + dx - PAD : j_hi + dx - PAD, :],
-                    in1=by_tap[:, lo:hi, :, j_lo:j_hi, dx]
-                    .unsqueeze(4)
-                    .to_broadcast([P, hi - lo, B, j_hi - j_lo, SP]),
+                return by_tap[:, lo:hi, :, j_lo:j_hi, dx].unsqueeze(4).to_broadcast([P, hi - lo, B, j_hi - j_lo, width])
+
+            for dx in POOL_COLUMNS:
+                j_lo, j_hi = valid_positions(dx)
+                nc.gpsimd.tensor_tensor(
+                    out=prods[dx][i % PROD_SETS][:, 0 : hi - lo, :, j_lo:j_hi, :],
+                    in0=x3w[:, rows_in, :, j_lo + dx - PAD : j_hi + dx - PAD, :],
+                    in1=weights(dx, SP),
                     op=ALU.mult,
                 )
-                for dy in range(lo, hi):
-                    nc.tensor.matmul(
-                        out=acc[i][:],
-                        lhsT=prod[:, dy - lo].rearrange("p b j s -> p (b j s)"),
-                        rhs=ident[:],
-                        is_transpose=True,
-                        start=(dx == 0 and dy == lo),
-                        stop=(dx == WIN - 1 and dy == hi - 1),
+            add_up(bias_prods[i % PROD_SETS][:])
+            for dx in range(WIN):
+                if dx in POOL_COLUMNS:
+                    continue
+                j_lo, j_hi = valid_positions(dx)
+                for k in range(SP // PER_BANK):
+                    nc.vector.tensor_tensor(
+                        out=prods[dx][i % PROD_SETS][:, 0 : hi - lo, :, j_lo:j_hi, PER_BANK * k : PER_BANK * (k + 1)],
+                        in0=x3_rows[k][:, rows_in, :, j_lo + dx - PAD : j_hi + dx - PAD, :],
+                        in1=weights(dx, PER_BANK),
+                        op=ALU.mult,
                     )
+                for d in range(hi - lo):
+                    add_up(prods[dx][i % PROD_SETS][:, d])
+            for dx in POOL_COLUMNS:
+                for d in range(hi - lo):
+                    add_up(prods[dx][i % PROD_SETS][:, d])
 
         def finish(i):
             acc_sb = row_pool.tile([P, P], F32)
             nc.scalar.copy(out=acc_sb[:], in_=acc[i][:])
             num = num_pool.tile([P, B, SIDE, SP], F32)
             nc.tensor.transpose(num[:].rearrange("p b j s -> p (b j s)"), acc_sb[:], ident[:])
-            nc.vector.reciprocal(out=rden[:, i], in_=den[:, i])
             nc.vector.tensor_tensor(
                 out=out_sb[:, :, :, i, :],
                 in0=num[:].rearrange("p b j s -> p b s j"),
@@ -262,13 +290,15 @@ def tile_sam_pb_s_kernel(tc, logits, x, w3c_words, w3c_scales, b3c, out):
 
         def rows():
             numerators(0)
+            fold(0)
             for i in range(SIDE):
                 if i + 1 < SIDE:
                     numerators(i + 1)
-                fold(i)
                 weigh(i)
                 if i > 0:
                     finish(i - 1)
+                if i + 1 < SIDE:
+                    fold(i + 1)
             finish(SIDE - 1)
 
         rows()

@@ -34,7 +34,7 @@ PER_BANK = 4
 E_PITCH = WIDE + 1
 E_BLOCK = SIDE * E_PITCH
 PROD_SETS = 2
-POOL_COLUMNS = (2, 4)
+POOL_COLUMNS = (0, WIN - 1)
 
 FLOPS = 2 * B * HW * CIN * COUT + 2 * B * COUT * HW * TAPS
 
@@ -75,7 +75,7 @@ def tile_sam_pb_s_kernel(tc, logits, x, w3c_words, w3c_scales, b3c, out):
         for dx in range(WIN):
             j_lo, j_hi = valid_positions(dx)
             sets = []
-            for k in range(PROD_SETS):
+            for k in range(0 if dx in POOL_COLUMNS else PROD_SETS):
                 prod = keep.tile([P, WIN, B, SIDE, SP], F32, name="prod%d_%d" % (dx, k))
                 if j_lo > 0:
                     nc.gpsimd.memset(prod[:, :, :, 0:j_lo, :], 0.0)
@@ -84,6 +84,8 @@ def tile_sam_pb_s_kernel(tc, logits, x, w3c_words, w3c_scales, b3c, out):
                 sets.append(prod)
             prods.append(sets)
 
+        outer_prods = [keep.tile([P, WIN, B, SIDE, SP], F32, name="outer_prod%d" % k) for k in range(PROD_SETS)]
+        spare_prods = [keep.tile([P, WIN, B, SIDE - 2 * PAD, SP], F32, name="spare_prod%d" % k) for k in range(PROD_SETS)]
         bias_prods = [keep.tile([P, B, SIDE, SP], F32, name="bias_prod%d" % k) for k in range(PROD_SETS)]
 
         x_raw = keep.tile([P, B, PASSES, PACK, HW], BF16)
@@ -233,7 +235,8 @@ def tile_sam_pb_s_kernel(tc, logits, x, w3c_words, w3c_scales, b3c, out):
             rows_in = slice(i + lo - PAD, i + hi - PAD)
             by_tap = e[:, i].rearrange("p d b (j c) -> p d b j c", c=E_PITCH)
             acc[i] = acc_pool.tile([P, P], F32, name="acc")
-            left = [1 + WIN * (hi - lo)]
+            blocks = 1 + (WIN - 1) * (hi - lo)
+            left = [blocks]
 
             def add_up(block):
                 nc.tensor.matmul(
@@ -241,23 +244,33 @@ def tile_sam_pb_s_kernel(tc, logits, x, w3c_words, w3c_scales, b3c, out):
                     lhsT=block.rearrange("p b j s -> p (b j s)"),
                     rhs=ident[:],
                     is_transpose=True,
-                    start=(left[0] == 1 + WIN * (hi - lo)),
+                    start=(left[0] == blocks),
                     stop=(left[0] == 1),
                 )
                 left[0] -= 1
 
-            def weights(dx, width):
-                j_lo, j_hi = valid_positions(dx)
+            def weights(dx, j_lo, j_hi, width):
                 return by_tap[:, lo:hi, :, j_lo:j_hi, dx].unsqueeze(4).to_broadcast([P, hi - lo, B, j_hi - j_lo, width])
 
-            for dx in POOL_COLUMNS:
-                j_lo, j_hi = valid_positions(dx)
+            def pool_product(target, dx, j_lo, j_hi):
                 nc.gpsimd.tensor_tensor(
-                    out=prods[dx][i % PROD_SETS][:, 0 : hi - lo, :, j_lo:j_hi, :],
+                    out=target,
                     in0=x3w[:, rows_in, :, j_lo + dx - PAD : j_hi + dx - PAD, :],
-                    in1=weights(dx, SP),
+                    in1=weights(dx, j_lo, j_hi, SP),
                     op=ALU.mult,
                 )
+
+            first, last = POOL_COLUMNS
+            first_lo, first_hi = valid_positions(first)
+            last_lo, last_hi = valid_positions(last)
+            outer = outer_prods[i % PROD_SETS][:, 0 : hi - lo]
+            spare = spare_prods[i % PROD_SETS][:, 0 : hi - lo]
+            pool_product(outer[:, :, :, first_lo:first_hi, :], first, first_lo, first_hi)
+            pool_product(outer[:, :, :, last_lo:first_lo, :], last, last_lo, first_lo)
+            pool_product(spare, last, first_lo, last_hi)
+            nc.gpsimd.tensor_tensor(
+                out=outer[:, :, :, first_lo:last_hi, :], in0=outer[:, :, :, first_lo:last_hi, :], in1=spare, op=ALU.add
+            )
             add_up(bias_prods[i % PROD_SETS][:])
             for dx in range(WIN):
                 if dx in POOL_COLUMNS:
@@ -267,14 +280,13 @@ def tile_sam_pb_s_kernel(tc, logits, x, w3c_words, w3c_scales, b3c, out):
                     nc.vector.tensor_tensor(
                         out=prods[dx][i % PROD_SETS][:, 0 : hi - lo, :, j_lo:j_hi, PER_BANK * k : PER_BANK * (k + 1)],
                         in0=x3_rows[k][:, rows_in, :, j_lo + dx - PAD : j_hi + dx - PAD, :],
-                        in1=weights(dx, PER_BANK),
+                        in1=weights(dx, j_lo, j_hi, PER_BANK),
                         op=ALU.mult,
                     )
                 for d in range(hi - lo):
                     add_up(prods[dx][i % PROD_SETS][:, d])
-            for dx in POOL_COLUMNS:
-                for d in range(hi - lo):
-                    add_up(prods[dx][i % PROD_SETS][:, d])
+            for d in range(hi - lo):
+                add_up(outer[:, d])
 
         def finish(i):
             acc_sb = row_pool.tile([P, P], F32)

@@ -64,6 +64,9 @@ def tile_sam_pb_s_kernel(tc, logits, x, w3c_words, w3c_scales, b3c, out):
 
         ident = keep.tile([P, P], F32)
         make_identity(nc, ident[:])
+        warm = keep.tile([P, 2], F32)
+        nc.vector.memset(warm[:], 0.0)
+        nc.scalar.activation(out=warm[:, 1:2], in_=warm[:, 0:1], func=ACT.Exp)
         w_scales = keep.tile([P, PASSES, COUT], U8, align_bytes=64)
         nc.vector.memset(w_scales[:].bitcast(I32), 0)
 
@@ -88,6 +91,13 @@ def tile_sam_pb_s_kernel(tc, logits, x, w3c_words, w3c_scales, b3c, out):
         spare_prods = [keep.tile([P, WIN, B, SIDE - 2 * PAD, SP], F32, name="spare_prod%d" % k) for k in range(PROD_SETS)]
         bias_prods = [keep.tile([P, B, SIDE, SP], F32, name="bias_prod%d" % k) for k in range(PROD_SETS)]
 
+        for quad in range(4):
+            nc.sync.dma_start(
+                out=w_scales[32 * quad : 32 * quad + 4].bitcast(I32),
+                in_=w3c_scales[:, 4 * quad : 4 * quad + 4, :].bitcast(I32).rearrange("g r n -> r g n"),
+            )
+        bias = keep.tile([P, SP], BF16)
+        nc.sync.dma_start(out=bias[:], in_=b3c.rearrange("(h s) -> h s", s=SP))
         x_raw = keep.tile([P, B, PASSES, PACK, HW], BF16)
         nc.sync.dma_start(
             out=x_raw[:].rearrange("p b g t n -> p b g (t n)"),
@@ -100,17 +110,12 @@ def tile_sam_pb_s_kernel(tc, logits, x, w3c_words, w3c_scales, b3c, out):
                 in_=logits[b].rearrange("h l n -> h (l n)"),
             )
         w_words = keep.tile([P, PASSES, 2 * COUT], U8, align_bytes=64)
-        nc.sync.dma_start(
-            out=w_words[:].bitcast(I32),
-            in_=w3c_words.bitcast(I32).rearrange("g p w -> p g w"),
-        )
-        for quad in range(4):
+        for half in range(HALVES):
+            cols = slice(2 * N_HALF * half, 2 * N_HALF * (half + 1))
             nc.sync.dma_start(
-                out=w_scales[32 * quad : 32 * quad + 4].bitcast(I32),
-                in_=w3c_scales[:, 4 * quad : 4 * quad + 4, :].bitcast(I32).rearrange("g r n -> r g n"),
+                out=w_words[:, :, cols].bitcast(I32),
+                in_=w3c_words[:, :, cols].bitcast(I32).rearrange("g p w -> p g w"),
             )
-        bias = keep.tile([P, SP], BF16)
-        nc.sync.dma_start(out=bias[:], in_=b3c.rearrange("(h s) -> h s", s=SP))
 
         grouped = keep.tile([P, PASSES, SIDE, B, SIDE, PACK], BF16, align_bytes=64)
         for g in range(PASSES):
@@ -124,27 +129,42 @@ def tile_sam_pb_s_kernel(tc, logits, x, w3c_words, w3c_scales, b3c, out):
             in_=grouped[:].rearrange("p g i b j t -> p (g i b j t)"),
         )
 
-        taps = [lg[:, b].rearrange("p u v i j -> p (u v) (i j)") for b in range(B)]
-        level = [taps[b][:, 0 : TAPS - 1, :] for b in range(B)]
-        for span in (24, 12, 6, 3):
-            for b in range(B):
-                nxt = keep.tile([P, span, HW], BF16, name="max%d_%d" % (span, b))
-                nc.vector.tensor_tensor(
-                    out=nxt[:], in0=level[b][:, 0:span, :], in1=level[b][:, span : 2 * span, :], op=ALU.max
-                )
-                level[b] = nxt[:]
-        peak = keep.tile([P, B, HW], BF16)
         neg_peak = keep.tile([P, B, SIDE, SIDE], F32)
         for b in range(B):
-            nc.vector.tensor_tensor(out=peak[:, b], in0=level[b][:, 0, :], in1=level[b][:, 1, :], op=ALU.max)
-        for b in range(B):
-            nc.vector.tensor_tensor(out=peak[:, b], in0=peak[:, b], in1=level[b][:, 2, :], op=ALU.max)
-        for b in range(B):
-            nc.vector.tensor_tensor(out=peak[:, b], in0=peak[:, b], in1=taps[b][:, TAPS - 1, :], op=ALU.max)
-        for b in range(B):
-            nc.vector.tensor_scalar_mul(
-                out=neg_peak[:, b].rearrange("p i j -> p (i j)"), in0=peak[:, b], scalar1=-1.0
+            win_rows = lg[:, b].rearrange("p u v i j -> p u (v i j)")
+            pairs = keep.tile([P, WIN // 2, WIN * HW], BF16, name="pairs%d" % b)
+            nc.vector.tensor_tensor(
+                out=pairs[:], in0=win_rows[:, 0 : WIN - 1 : 2, :], in1=win_rows[:, 1 : WIN - 1 : 2, :], op=ALU.max
             )
+            fours = keep.tile([P, 2, WIN * HW], BF16, name="fours%d" % b)
+            nc.vector.tensor_tensor(out=fours[:, 0], in0=pairs[:, 0], in1=pairs[:, 1], op=ALU.max)
+            nc.vector.tensor_tensor(out=fours[:, 1], in0=pairs[:, 2], in1=win_rows[:, WIN - 1, :], op=ALU.max)
+            sevens = keep.tile([P, WIN, HW], BF16, name="sevens%d" % b)
+            nc.vector.tensor_tensor(
+                out=sevens[:].rearrange("p v n -> p (v n)"), in0=fours[:, 0], in1=fours[:, 1], op=ALU.max
+            )
+            nc.vector.tensor_reduce(
+                out=neg_peak[:, b].rearrange("p i j -> p (i j)"),
+                in_=sevens[:].rearrange("p v n -> p n v"),
+                axis=mybir.AxisListType.X,
+                op=ALU.max,
+                negate=True,
+            )
+
+        den = keep.tile([P, SIDE, B, SIDE], F32)
+
+        def numerators(i):
+            for b in range(B):
+                for j in range(SIDE):
+                    nc.scalar.activation(
+                        out=e[:, i, :, b, E_PITCH * j : E_PITCH * j + WIN],
+                        in_=lg[:, b, :, :, i, j],
+                        func=ACT.Exp,
+                        bias=neg_peak[:, b, i, j : j + 1],
+                        accum_out=den[:, i, b, j : j + 1],
+                    )
+
+        numerators(0)
 
         x3_pos = keep.tile([P, SP, HEADS], F32)
         heads_half = N_HALF // SP
@@ -160,7 +180,7 @@ def tile_sam_pb_s_kernel(tc, logits, x, w3c_words, w3c_scales, b3c, out):
                     start=(g == 0),
                     stop=(g == PASSES - 1),
                 )
-            nc.scalar.copy(
+            nc.vector.tensor_copy(
                 out=x3_pos[:, :, heads_half * half : heads_half * (half + 1)],
                 in_=proj[:].rearrange("p (h s) -> p s h", s=SP),
             )
@@ -172,23 +192,12 @@ def tile_sam_pb_s_kernel(tc, logits, x, w3c_words, w3c_scales, b3c, out):
             for q in range(PER_BANK):
                 nc.tensor.transpose(x3_head[:, q, :], x3_pos[:, PER_BANK * k + q, :], ident[:])
             x3_rows.append(x3_head[:].rearrange("p s (i b j) -> p i b j s", b=B, i=SIDE))
-            nc.vector.tensor_copy(out=x3w[:, :, :, :, PER_BANK * k : PER_BANK * (k + 1)], in_=x3_rows[k])
+        nc.vector.tensor_copy(out=x3w[:, :, :, :, 0:PER_BANK], in_=x3_rows[0])
+        nc.scalar.copy(out=x3w[:, :, :, :, PER_BANK:SP], in_=x3_rows[1])
 
-        den = keep.tile([P, SIDE, B, SIDE], F32)
         rden = keep.tile([P, SIDE, B, SIDE], F32)
         out_sb = keep.tile([P, B, SP, SIDE, SIDE], F32)
         acc = {}
-
-        def numerators(i):
-            for b in range(B):
-                for j in range(SIDE):
-                    nc.scalar.activation(
-                        out=e[:, i, :, b, E_PITCH * j : E_PITCH * j + WIN],
-                        in_=lg[:, b, :, :, i, j],
-                        func=ACT.Exp,
-                        bias=neg_peak[:, b, i, j : j + 1],
-                        accum_out=den[:, i, b, j : j + 1],
-                    )
 
         def fold(i):
             lo, hi = valid_taps(i)
@@ -222,6 +231,8 @@ def tile_sam_pb_s_kernel(tc, logits, x, w3c_words, w3c_scales, b3c, out):
                 in1=by_col[:, lo:hi, :, SIDE - PAD : SIDE, WIDE - 1 : WIDE - PAD - 1 : -1],
                 op=ALU.add,
             )
+
+        def extras(i):
             nc.vector.tensor_tensor(
                 out=bias_prods[i % PROD_SETS][:],
                 in0=den[:, i].unsqueeze(3).to_broadcast([P, B, SIDE, SP]),
@@ -271,7 +282,6 @@ def tile_sam_pb_s_kernel(tc, logits, x, w3c_words, w3c_scales, b3c, out):
             nc.gpsimd.tensor_tensor(
                 out=outer[:, :, :, first_lo:last_hi, :], in0=outer[:, :, :, first_lo:last_hi, :], in1=spare, op=ALU.add
             )
-            add_up(bias_prods[i % PROD_SETS][:])
             for dx in range(WIN):
                 if dx in POOL_COLUMNS:
                     continue
@@ -287,6 +297,9 @@ def tile_sam_pb_s_kernel(tc, logits, x, w3c_words, w3c_scales, b3c, out):
                     add_up(prods[dx][i % PROD_SETS][:, d])
             for d in range(hi - lo):
                 add_up(outer[:, d])
+            if i == 0:
+                extras(0)
+            add_up(bias_prods[i % PROD_SETS][:])
 
         def finish(i):
             acc_sb = row_pool.tile([P, P], F32)
@@ -301,7 +314,6 @@ def tile_sam_pb_s_kernel(tc, logits, x, w3c_words, w3c_scales, b3c, out):
             )
 
         def rows():
-            numerators(0)
             fold(0)
             for i in range(SIDE):
                 if i + 1 < SIDE:
@@ -311,6 +323,7 @@ def tile_sam_pb_s_kernel(tc, logits, x, w3c_words, w3c_scales, b3c, out):
                     finish(i - 1)
                 if i + 1 < SIDE:
                     fold(i + 1)
+                    extras(i + 1)
             finish(SIDE - 1)
 
         rows()

@@ -289,8 +289,8 @@ def tile_sam_pb_s_kernel(tc, logits, x, w3c_words, w3c_scales, b3c, out):
                 for k in range(SP // PER_BANK):
                     nc.vector.tensor_tensor(
                         out=prods[dx][i % PROD_SETS][:, 0 : hi - lo, :, j_lo:j_hi, PER_BANK * k : PER_BANK * (k + 1)],
-                        in0=x3_rows[k][:, rows_in, :, j_lo + dx - PAD : j_hi + dx - PAD, :],
-                        in1=weights(dx, j_lo, j_hi, PER_BANK),
+                        in0=weights(dx, j_lo, j_hi, PER_BANK),
+                        in1=x3_rows[k][:, rows_in, :, j_lo + dx - PAD : j_hi + dx - PAD, :],
                         op=ALU.mult,
                     )
                 for d in range(hi - lo):
@@ -308,8 +308,8 @@ def tile_sam_pb_s_kernel(tc, logits, x, w3c_words, w3c_scales, b3c, out):
             nc.tensor.transpose(num[:].rearrange("p b j s -> p (b j s)"), acc_sb[:], ident[:])
             nc.vector.tensor_tensor(
                 out=out_sb[:, :, :, i, :],
-                in0=num[:].rearrange("p b j s -> p b s j"),
-                in1=rden[:, i].unsqueeze(2).to_broadcast([P, B, SP, SIDE]),
+                in0=rden[:, i].unsqueeze(2).to_broadcast([P, B, SP, SIDE]),
+                in1=num[:].rearrange("p b j s -> p b s j"),
                 op=ALU.mult,
             )
 

@@ -31,7 +31,7 @@ PASSES = CIN // K_PASS
 N_HALF = 512
 HALVES = COUT // N_HALF
 PER_BANK = 4
-E_PITCH = WIDE + 1
+E_PITCH = 16
 E_BLOCK = SIDE * E_PITCH
 PROD_SETS = 2
 POOL_COLUMNS = (0, WIN - 1)
@@ -89,7 +89,6 @@ def tile_sam_pb_s_kernel(tc, logits, x, w3c_words, w3c_scales, b3c, out):
 
         outer_prods = [keep.tile([P, WIN, B, SIDE, SP], F32, name="outer_prod%d" % k) for k in range(PROD_SETS)]
         spare_prods = [keep.tile([P, WIN, B, SIDE - 2 * PAD, SP], F32, name="spare_prod%d" % k) for k in range(PROD_SETS)]
-        bias_prods = [keep.tile([P, B, SIDE, SP], F32, name="bias_prod%d" % k) for k in range(PROD_SETS)]
 
         for quad in range(4):
             nc.sync.dma_start(
@@ -129,6 +128,16 @@ def tile_sam_pb_s_kernel(tc, logits, x, w3c_words, w3c_scales, b3c, out):
             in_=grouped[:].rearrange("p g i b j t -> p (g i b j t)"),
         )
 
+        bias_f32 = keep.tile([P, SP], F32)
+        nc.vector.tensor_copy(out=bias_f32[:], in_=bias[:])
+        bias_pos = keep.tile([P, SP, HEADS], F32)
+        for k in range(SP // PER_BANK):
+            spread = psum.tile([P, PER_BANK, P], F32, tag="head%d" % k)
+            for q in range(PER_BANK):
+                s = PER_BANK * k + q
+                nc.tensor.transpose(spread[:, q, :], bias_f32[:, s : s + 1].to_broadcast([P, P]), ident[:])
+            nc.scalar.copy(out=bias_pos[:, PER_BANK * k : PER_BANK * (k + 1), :], in_=spread[:])
+
         neg_peak = keep.tile([P, B, SIDE, SIDE], F32)
         for b in range(B):
             win_rows = lg[:, b].rearrange("p u v i j -> p u (v i j)")
@@ -166,39 +175,6 @@ def tile_sam_pb_s_kernel(tc, logits, x, w3c_words, w3c_scales, b3c, out):
 
         numerators(0)
 
-        x3_pos = keep.tile([P, SP, HEADS], F32)
-        heads_half = N_HALF // SP
-        for half in range(HALVES):
-            proj = psum.tile([P, N_HALF], F32, tag="proj%d" % half)
-            for g in range(PASSES):
-                nc.tensor.matmul_mx(
-                    out=proj[:],
-                    lhsT=x_codes[:, g * P : (g + 1) * P].bitcast(FP8X4),
-                    lhsT_scale=x_scales[:, g * P : (g + 1) * P],
-                    rhs=w_words[:, g, 2 * N_HALF * half : 2 * N_HALF * (half + 1)].bitcast(FP4X4),
-                    rhs_scale=w_scales[:, g, N_HALF * half : N_HALF * (half + 1)],
-                    start=(g == 0),
-                    stop=(g == PASSES - 1),
-                )
-            nc.vector.tensor_copy(
-                out=x3_pos[:, :, heads_half * half : heads_half * (half + 1)],
-                in_=proj[:].rearrange("p (h s) -> p s h", s=SP),
-            )
-
-        x3w = keep.tile([P, SIDE, B, SIDE, SP], F32)
-        x3_rows = []
-        for k in range(SP // PER_BANK):
-            x3_head = psum.tile([P, PER_BANK, P], F32, tag="head%d" % k)
-            for q in range(PER_BANK):
-                nc.tensor.transpose(x3_head[:, q, :], x3_pos[:, PER_BANK * k + q, :], ident[:])
-            x3_rows.append(x3_head[:].rearrange("p s (i b j) -> p i b j s", b=B, i=SIDE))
-        nc.vector.tensor_copy(out=x3w[:, :, :, :, 0:PER_BANK], in_=x3_rows[0])
-        nc.scalar.copy(out=x3w[:, :, :, :, PER_BANK:SP], in_=x3_rows[1])
-
-        rden = keep.tile([P, SIDE, B, SIDE], F32)
-        out_sb = keep.tile([P, B, SP, SIDE, SIDE], F32)
-        acc = {}
-
         def fold(i):
             lo, hi = valid_taps(i)
             by_tap = e[:, i].rearrange("p d b (j c) -> p d b j c", c=E_PITCH)
@@ -218,7 +194,7 @@ def tile_sam_pb_s_kernel(tc, logits, x, w3c_words, w3c_scales, b3c, out):
                     in1=by_tap[:, WIN - 1 : hi - 1 : -1, :, :, 0:WIN],
                     op=ALU.add,
                 )
-            by_col = e[:, i, :, :, 0 : SIDE * WIDE].rearrange("p d b (j c) -> p d b j c", c=WIDE)
+            by_col = e[:, i, :, :, 0 : SIDE * (E_PITCH - 1)].rearrange("p d b (j c) -> p d b j c", c=E_PITCH - 1)
             nc.vector.tensor_tensor(
                 out=by_col[:, lo:hi, :, 0:PAD, PAD + 1 : 2 * PAD + 1],
                 in0=by_col[:, lo:hi, :, 0:PAD, PAD + 1 : 2 * PAD + 1],
@@ -232,13 +208,44 @@ def tile_sam_pb_s_kernel(tc, logits, x, w3c_words, w3c_scales, b3c, out):
                 op=ALU.add,
             )
 
-        def extras(i):
+        fold(0)
+
+        x3_pos = keep.tile([P, SP, HEADS], F32)
+        heads_half = N_HALF // SP
+        for half in range(HALVES):
+            proj = psum.tile([P, N_HALF], F32, tag="proj%d" % half)
+            for g in range(PASSES):
+                nc.tensor.matmul_mx(
+                    out=proj[:],
+                    lhsT=x_codes[:, g * P : (g + 1) * P].bitcast(FP8X4),
+                    lhsT_scale=x_scales[:, g * P : (g + 1) * P],
+                    rhs=w_words[:, g, 2 * N_HALF * half : 2 * N_HALF * (half + 1)].bitcast(FP4X4),
+                    rhs_scale=w_scales[:, g, N_HALF * half : N_HALF * (half + 1)],
+                    start=(g == 0),
+                    stop=(g == PASSES - 1),
+                )
             nc.vector.tensor_tensor(
-                out=bias_prods[i % PROD_SETS][:],
-                in0=den[:, i].unsqueeze(3).to_broadcast([P, B, SIDE, SP]),
-                in1=bias[:].unsqueeze(1).unsqueeze(1).to_broadcast([P, B, SIDE, SP]),
-                op=ALU.mult,
+                out=x3_pos[:, :, heads_half * half : heads_half * (half + 1)],
+                in0=bias_pos[:, :, heads_half * half : heads_half * (half + 1)],
+                in1=proj[:].rearrange("p (h s) -> p s h", s=SP),
+                op=ALU.add,
             )
+
+        x3w = keep.tile([P, SIDE, B, SIDE, SP], F32)
+        x3_rows = []
+        for k in range(SP // PER_BANK):
+            x3_head = psum.tile([P, PER_BANK, P], F32, tag="head%d" % k)
+            for q in range(PER_BANK):
+                nc.tensor.transpose(x3_head[:, q, :], x3_pos[:, PER_BANK * k + q, :], ident[:])
+            x3_rows.append(x3_head[:].rearrange("p s (i b j) -> p i b j s", b=B, i=SIDE))
+        nc.vector.tensor_copy(out=x3w[:, :, :, :, 0:PER_BANK], in_=x3_rows[0])
+        nc.scalar.copy(out=x3w[:, :, :, :, PER_BANK:SP], in_=x3_rows[1])
+
+        rden = keep.tile([P, SIDE, B, SIDE], F32)
+        out_sb = keep.tile([P, B, SP, SIDE, SIDE], F32)
+        acc = {}
+
+        def extras(i):
             nc.vector.reciprocal(out=rden[:, i], in_=den[:, i])
 
         def weigh(i):
@@ -246,7 +253,7 @@ def tile_sam_pb_s_kernel(tc, logits, x, w3c_words, w3c_scales, b3c, out):
             rows_in = slice(i + lo - PAD, i + hi - PAD)
             by_tap = e[:, i].rearrange("p d b (j c) -> p d b j c", c=E_PITCH)
             acc[i] = acc_pool.tile([P, P], F32, name="acc")
-            blocks = 1 + (WIN - 1) * (hi - lo)
+            blocks = (WIN - 1) * (hi - lo)
             left = [blocks]
 
             def add_up(block):
@@ -299,7 +306,6 @@ def tile_sam_pb_s_kernel(tc, logits, x, w3c_words, w3c_scales, b3c, out):
                 add_up(outer[:, d])
             if i == 0:
                 extras(0)
-            add_up(bias_prods[i % PROD_SETS][:])
 
         def finish(i):
             acc_sb = row_pool.tile([P, P], F32)
@@ -314,7 +320,6 @@ def tile_sam_pb_s_kernel(tc, logits, x, w3c_words, w3c_scales, b3c, out):
             )
 
         def rows():
-            fold(0)
             for i in range(SIDE):
                 if i + 1 < SIDE:
                     numerators(i + 1)

@@ -34,6 +34,9 @@ PER_BANK = 4
 E_PITCH = 16
 E_BLOCK = SIDE * E_PITCH
 PROD_SETS = 2
+SCALAR_COLUMN = PAD
+SCALAR_FROM = SIDE - 2
+SCALAR_FIRST_ROW = 1
 POOL_COLUMNS = (0, WIN - 1)
 
 FLOPS = 2 * B * HW * CIN * COUT + 2 * B * COUT * HW * TAPS
@@ -139,28 +142,32 @@ def tile_sam_pb_s_kernel(tc, logits, x, w3c_words, w3c_scales, b3c, out):
             nc.scalar.copy(out=bias_pos[:, PER_BANK * k : PER_BANK * (k + 1), :], in_=spread[:])
 
         neg_peak = keep.tile([P, B, SIDE, SIDE], F32)
-        for b in range(B):
-            win_rows = lg[:, b].rearrange("p u v i j -> p u (v i j)")
-            pairs = keep.tile([P, WIN // 2, WIN * HW], BF16, name="pairs%d" % b)
+
+        def peaks(b, rows):
+            count = rows.stop - rows.start
+            win_rows = lg[:, b, :, :, rows].rearrange("p u v i j -> p u v (i j)")
+            name = "%d_%d" % (b, rows.start)
+            pairs = keep.tile([P, WIN // 2, WIN, count * SIDE], BF16, name="pairs" + name)
             nc.vector.tensor_tensor(
-                out=pairs[:], in0=win_rows[:, 0 : WIN - 1 : 2, :], in1=win_rows[:, 1 : WIN - 1 : 2, :], op=ALU.max
+                out=pairs[:], in0=win_rows[:, 0 : WIN - 1 : 2], in1=win_rows[:, 1 : WIN - 1 : 2], op=ALU.max
             )
-            fours = keep.tile([P, 2, WIN * HW], BF16, name="fours%d" % b)
+            fours = keep.tile([P, 2, WIN, count * SIDE], BF16, name="fours" + name)
             nc.vector.tensor_tensor(out=fours[:, 0], in0=pairs[:, 0], in1=pairs[:, 1], op=ALU.max)
-            nc.vector.tensor_tensor(out=fours[:, 1], in0=pairs[:, 2], in1=win_rows[:, WIN - 1, :], op=ALU.max)
-            sevens = keep.tile([P, WIN, HW], BF16, name="sevens%d" % b)
-            nc.vector.tensor_tensor(
-                out=sevens[:].rearrange("p v n -> p (v n)"), in0=fours[:, 0], in1=fours[:, 1], op=ALU.max
-            )
+            nc.vector.tensor_tensor(out=fours[:, 1], in0=pairs[:, 2], in1=win_rows[:, WIN - 1], op=ALU.max)
+            sevens = keep.tile([P, WIN, count * SIDE], BF16, name="sevens" + name)
+            nc.vector.tensor_tensor(out=sevens[:], in0=fours[:, 0], in1=fours[:, 1], op=ALU.max)
             nc.vector.tensor_reduce(
-                out=neg_peak[:, b].rearrange("p i j -> p (i j)"),
+                out=neg_peak[:, b, rows].rearrange("p i j -> p (i j)"),
                 in_=sevens[:].rearrange("p v n -> p n v"),
                 axis=mybir.AxisListType.X,
                 op=ALU.max,
                 negate=True,
             )
 
-        den = keep.tile([P, SIDE, B, SIDE], F32)
+        for b in range(B):
+            peaks(b, slice(0, 1))
+
+        den = keep.tile([P, B, SIDE, SIDE], F32)
 
         def numerators(i):
             for b in range(B):
@@ -170,10 +177,12 @@ def tile_sam_pb_s_kernel(tc, logits, x, w3c_words, w3c_scales, b3c, out):
                         in_=lg[:, b, :, :, i, j],
                         func=ACT.Exp,
                         bias=neg_peak[:, b, i, j : j + 1],
-                        accum_out=den[:, i, b, j : j + 1],
+                        accum_out=den[:, b, i, j : j + 1],
                     )
 
         numerators(0)
+        for b in range(B):
+            peaks(b, slice(1, SIDE))
 
         def fold(i):
             lo, hi = valid_taps(i)
@@ -238,15 +247,15 @@ def tile_sam_pb_s_kernel(tc, logits, x, w3c_words, w3c_scales, b3c, out):
             for q in range(PER_BANK):
                 nc.tensor.transpose(x3_head[:, q, :], x3_pos[:, PER_BANK * k + q, :], ident[:])
             x3_rows.append(x3_head[:].rearrange("p s (i b j) -> p i b j s", b=B, i=SIDE))
-        nc.vector.tensor_copy(out=x3w[:, :, :, :, 0:PER_BANK], in_=x3_rows[0])
-        nc.scalar.copy(out=x3w[:, :, :, :, PER_BANK:SP], in_=x3_rows[1])
+        for k in range(SP // PER_BANK):
+            nc.scalar.copy(out=x3w[:, :, :, :, PER_BANK * k : PER_BANK * (k + 1)], in_=x3_rows[k])
 
-        rden = keep.tile([P, SIDE, B, SIDE], F32)
+        rden = keep.tile([P, B, SIDE, SIDE], F32)
         out_sb = keep.tile([P, B, SP, SIDE, SIDE], F32)
         acc = {}
 
-        def extras(i):
-            nc.vector.reciprocal(out=rden[:, i], in_=den[:, i])
+        def invert(rows):
+            nc.vector.reciprocal(out=rden[:, :, rows], in_=den[:, :, rows])
 
         def weigh(i):
             lo, hi = valid_taps(i)
@@ -289,10 +298,20 @@ def tile_sam_pb_s_kernel(tc, logits, x, w3c_words, w3c_scales, b3c, out):
             nc.gpsimd.tensor_tensor(
                 out=outer[:, :, :, first_lo:last_hi, :], in0=outer[:, :, :, first_lo:last_hi, :], in1=spare, op=ALU.add
             )
-            for dx in range(WIN):
-                if dx in POOL_COLUMNS:
-                    continue
+            scalar_from = SCALAR_FROM if i >= SCALAR_FIRST_ROW else SIDE
+            for d in range(hi - lo):
+                for b in range(B):
+                    for j in range(scalar_from, SIDE):
+                        nc.scalar.activation(
+                            out=prods[SCALAR_COLUMN][i % PROD_SETS][:, d, b, j, :],
+                            in_=x3w[:, i + lo + d - PAD, b, j, :],
+                            func=ACT.Copy,
+                            scale=by_tap[:, lo + d, b, j, SCALAR_COLUMN : SCALAR_COLUMN + 1],
+                        )
+            for dx in [dx for dx in range(WIN) if dx not in POOL_COLUMNS and dx != SCALAR_COLUMN] + [SCALAR_COLUMN]:
                 j_lo, j_hi = valid_positions(dx)
+                if dx == SCALAR_COLUMN:
+                    j_hi = scalar_from
                 for k in range(SP // PER_BANK):
                     nc.vector.tensor_tensor(
                         out=prods[dx][i % PROD_SETS][:, 0 : hi - lo, :, j_lo:j_hi, PER_BANK * k : PER_BANK * (k + 1)],
@@ -304,18 +323,22 @@ def tile_sam_pb_s_kernel(tc, logits, x, w3c_words, w3c_scales, b3c, out):
                     add_up(prods[dx][i % PROD_SETS][:, d])
             for d in range(hi - lo):
                 add_up(outer[:, d])
-            if i == 0:
-                extras(0)
 
-        def finish(i):
+        num = {}
+
+        def turn_back(i):
             acc_sb = row_pool.tile([P, P], F32)
             nc.scalar.copy(out=acc_sb[:], in_=acc[i][:])
-            num = num_pool.tile([P, B, SIDE, SP], F32)
-            nc.tensor.transpose(num[:].rearrange("p b j s -> p (b j s)"), acc_sb[:], ident[:])
+            if i % 2 == 0:
+                num[i // 2] = num_pool.tile([P, B, 2 * SIDE, SP], F32, name="num")
+            row = num[i // 2][:, :, SIDE * (i % 2) : SIDE * (i % 2 + 1), :]
+            nc.tensor.transpose(row.rearrange("p b j s -> p b (j s)"), acc_sb[:], ident[:])
+
+        def divide(i):
             nc.vector.tensor_tensor(
-                out=out_sb[:, :, :, i, :],
-                in0=rden[:, i].unsqueeze(2).to_broadcast([P, B, SP, SIDE]),
-                in1=num[:].rearrange("p b j s -> p b s j"),
+                out=out_sb[:, :, :, i : i + 2, :].rearrange("p b s i j -> p b s (i j)"),
+                in0=rden[:, :, i : i + 2].rearrange("p b i j -> p b (i j)").unsqueeze(2).to_broadcast([P, B, SP, 2 * SIDE]),
+                in1=num[i // 2][:].rearrange("p b j s -> p b s j"),
                 op=ALU.mult,
             )
 
@@ -325,11 +348,17 @@ def tile_sam_pb_s_kernel(tc, logits, x, w3c_words, w3c_scales, b3c, out):
                     numerators(i + 1)
                 weigh(i)
                 if i > 0:
-                    finish(i - 1)
+                    turn_back(i - 1)
+                if i == 2:
+                    invert(slice(0, SIDE // 2))
+                if i == SIDE // 2 + 2:
+                    invert(slice(SIDE // 2, SIDE))
+                if i > 0 and i % 2 == 0:
+                    divide(i - 2)
                 if i + 1 < SIDE:
                     fold(i + 1)
-                    extras(i + 1)
-            finish(SIDE - 1)
+            turn_back(SIDE - 1)
+            divide(SIDE - 2)
 
         rows()
 

from contextlib import ExitStack

import concourse.mybir as mybir
from concourse.masks import make_identity

F32 = mybir.dt.float32
BF16 = mybir.dt.bfloat16
U8 = mybir.dt.uint8
U32 = mybir.dt.uint32
I32 = mybir.dt.int32
FP8X4 = mybir.dt.float8_e4m3fn_x4
FP4X4 = mybir.dt.float4_e2m1fn_x4
ALU = mybir.AluOpType
ACT = mybir.ActivationFunctionType

P = 128
B = 2
CIN = 1024
COUT = 1024
SIDE = 8
HW = SIDE * SIDE
SP = 8
HEADS = COUT // SP
WIN = 7
TAPS = WIN * WIN
PAD = WIN // 2
WIDE = SIDE + 2 * PAD
PACK = 4
K_PASS = P * PACK
PASSES = CIN // K_PASS
N_HALF = 512
HALVES = COUT // N_HALF
PER_BANK = 4
E_PITCH = 16
E_BLOCK = SIDE * E_PITCH
PROD_SETS = 2
SCALAR_COLUMN = PAD
SCALAR_FROM = SIDE - 2
SCALAR_FIRST_ROW = 1
POOL_COLUMNS = (0, WIN - 1)

FLOPS = 2 * B * HW * CIN * COUT + 2 * B * COUT * HW * TAPS


def valid_taps(i):
    return max(0, PAD - i), min(WIN, SIDE + PAD - i)


def reflected_tap(dy, i):
    u = i + dy - PAD
    source = -u if u < 0 else 2 * (SIDE - 1) - u
    return source - i + PAD


def valid_positions(dx):
    return max(0, PAD - dx), min(SIDE, SIDE + PAD - dx)


def tile_sam_pb_s_kernel(tc, logits, x, w3c_words, w3c_scales, b3c, out):
    nc = tc.nc
    with ExitStack() as ctx:
        keep = ctx.enter_context(tc.tile_pool(name="keep", bufs=1))
        row_pool = ctx.enter_context(tc.tile_pool(name="row", bufs=2))
        psum = ctx.enter_context(tc.psum_pool(name="psum", bufs=1))
        acc_pool = ctx.enter_context(tc.psum_pool(name="acc", bufs=2))
        num_pool = ctx.enter_context(tc.psum_pool(name="num", bufs=2))

        ident = keep.tile([P, P], F32)
        make_identity(nc, ident[:])
        warm = keep.tile([P, 2], F32)
        nc.vector.memset(warm[:], 0.0)
        nc.scalar.activation(out=warm[:, 1:2], in_=warm[:, 0:1], func=ACT.Exp)
        w_scales = keep.tile([P, PASSES, COUT], U8, align_bytes=64)
        nc.vector.memset(w_scales[:].bitcast(I32), 0)

        e = keep.tile([P, SIDE, WIN, B, E_BLOCK], F32)
        e_cells = e[:].rearrange("p i d b (j c) -> p (i d b) j c", c=E_PITCH)
        nc.vector.memset(e_cells[:, :, 0:2, E_PITCH - 2 : E_PITCH], 0.0)
        nc.vector.memset(e_cells[:, :, SIDE - 3 : SIDE - 1, WIN : WIN + 2], 0.0)
        prods = []
        for dx in range(WIN):
            j_lo, j_hi = valid_positions(dx)
            sets = []
            for k in range(0 if dx in POOL_COLUMNS else PROD_SETS):
                prod = keep.tile([P, WIN, B, SIDE, SP], F32, name="prod%d_%d" % (dx, k))
                if j_lo > 0:
                    nc.gpsimd.memset(prod[:, :, :, 0:j_lo, :], 0.0)
                if j_hi < SIDE:
                    nc.gpsimd.memset(prod[:, :, :, j_hi:SIDE, :], 0.0)
                sets.append(prod)
            prods.append(sets)

        outer_prods = [keep.tile([P, WIN, B, SIDE, SP], F32, name="outer_prod%d" % k) for k in range(PROD_SETS)]
        spare_prods = [keep.tile([P, WIN, B, SIDE - 2 * PAD, SP], F32, name="spare_prod%d" % k) for k in range(PROD_SETS)]

        for quad in range(4):
            nc.sync.dma_start(
                out=w_scales[32 * quad : 32 * quad + 4].bitcast(I32),
                in_=w3c_scales[:, 4 * quad : 4 * quad + 4, :].bitcast(I32).rearrange("g r n -> r g n"),
            )
        bias = keep.tile([P, SP], BF16)
        nc.sync.dma_start(out=bias[:], in_=b3c.rearrange("(h s) -> h s", s=SP))
        x_raw = keep.tile([P, B, PASSES, PACK, HW], BF16)
        nc.sync.dma_start(
            out=x_raw[:].rearrange("p b g t n -> p b g (t n)"),
            in_=x.rearrange("b (g p t) i j -> p b g (t i j)", g=PASSES, p=P, t=PACK),
        )
        lg = keep.tile([P, B, WIN, WIN, SIDE, SIDE], BF16)
        for b in range(B):
            nc.sync.dma_start(
                out=lg[:, b].rearrange("p u v i j -> p (u v i j)"),
                in_=logits[b].rearrange("h l n -> h (l n)"),
            )
        w_words = keep.tile([P, PASSES, 2 * COUT], U8, align_bytes=64)
        for half in range(HALVES):
            cols = slice(2 * N_HALF * half, 2 * N_HALF * (half + 1))
            nc.sync.dma_start(
                out=w_words[:, :, cols].bitcast(I32),
                in_=w3c_words[:, :, cols].bitcast(I32).rearrange("g p w -> p g w"),
            )

        grouped = keep.tile([P, PASSES, SIDE, B, SIDE, PACK], BF16, align_bytes=64)
        for g in range(PASSES):
            for b in range(B):
                nc.scalar.copy(out=grouped[:, g, :, b], in_=x_raw[:, b, g].rearrange("p t (i j) -> p i j t", i=SIDE))
        x_codes = keep.tile([P, PASSES * P], U32, align_bytes=64)
        x_scales = keep.tile([P, PASSES * P], U8, align_bytes=64)
        nc.vector.quantize_mx(
            out=x_codes[:].bitcast(FP8X4),
            scales=x_scales[:],
            in_=grouped[:].rearrange("p g i b j t -> p (g i b j t)"),
        )

        bias_f32 = keep.tile([P, SP], F32)
        nc.vector.tensor_copy(out=bias_f32[:], in_=bias[:])
        bias_pos = keep.tile([P, SP, HEADS], F32)
        for k in range(SP // PER_BANK):
            spread = psum.tile([P, PER_BANK, P], F32, tag="head%d" % k)
            for q in range(PER_BANK):
                s = PER_BANK * k + q
                nc.tensor.transpose(spread[:, q, :], bias_f32[:, s : s + 1].to_broadcast([P, P]), ident[:])
            nc.scalar.copy(out=bias_pos[:, PER_BANK * k : PER_BANK * (k + 1), :], in_=spread[:])

        neg_peak = keep.tile([P, B, SIDE, SIDE], F32)

        def peaks(b, rows):
            count = rows.stop - rows.start
            win_rows = lg[:, b, :, :, rows].rearrange("p u v i j -> p u v (i j)")
            name = "%d_%d" % (b, rows.start)
            pairs = keep.tile([P, WIN // 2, WIN, count * SIDE], BF16, name="pairs" + name)
            nc.vector.tensor_tensor(
                out=pairs[:], in0=win_rows[:, 0 : WIN - 1 : 2], in1=win_rows[:, 1 : WIN - 1 : 2], op=ALU.max
            )
            fours = keep.tile([P, 2, WIN, count * SIDE], BF16, name="fours" + name)
            nc.vector.tensor_tensor(out=fours[:, 0], in0=pairs[:, 0], in1=pairs[:, 1], op=ALU.max)
            nc.vector.tensor_tensor(out=fours[:, 1], in0=pairs[:, 2], in1=win_rows[:, WIN - 1], op=ALU.max)
            sevens = keep.tile([P, WIN, count * SIDE], BF16, name="sevens" + name)
            nc.vector.tensor_tensor(out=sevens[:], in0=fours[:, 0], in1=fours[:, 1], op=ALU.max)
            nc.vector.tensor_reduce(
                out=neg_peak[:, b, rows].rearrange("p i j -> p (i j)"),
                in_=sevens[:].rearrange("p v n -> p n v"),
                axis=mybir.AxisListType.X,
                op=ALU.max,
                negate=True,
            )

        for b in range(B):
            peaks(b, slice(0, 1))

        den = keep.tile([P, B, SIDE, SIDE], F32)

        def numerators(i):
            for b in range(B):
                for j in range(SIDE):
                    nc.scalar.activation(
                        out=e[:, i, :, b, E_PITCH * j : E_PITCH * j + WIN],
                        in_=lg[:, b, :, :, i, j],
                        func=ACT.Exp,
                        bias=neg_peak[:, b, i, j : j + 1],
                        accum_out=den[:, b, i, j : j + 1],
                    )

        numerators(0)
        for b in range(B):
            peaks(b, slice(1, SIDE))

        def fold(i):
            lo, hi = valid_taps(i)
            by_tap = e[:, i].rearrange("p d b (j c) -> p d b j c", c=E_PITCH)
            if lo > 0:
                onto = reflected_tap(lo - 1, i)
                nc.vector.tensor_tensor(
                    out=by_tap[:, onto : onto + lo, :, :, 0:WIN],
                    in0=by_tap[:, onto : onto + lo, :, :, 0:WIN],
                    in1=by_tap[:, lo - 1 :: -1, :, :, 0:WIN],
                    op=ALU.add,
                )
            if hi < WIN:
                onto = reflected_tap(WIN - 1, i)
                nc.vector.tensor_tensor(
                    out=by_tap[:, onto : onto + WIN - hi, :, :, 0:WIN],
                    in0=by_tap[:, onto : onto + WIN - hi, :, :, 0:WIN],
                    in1=by_tap[:, WIN - 1 : hi - 1 : -1, :, :, 0:WIN],
                    op=ALU.add,
                )
            by_col = e[:, i, :, :, 0 : SIDE * (E_PITCH - 1)].rearrange("p d b (j c) -> p d b j c", c=E_PITCH - 1)
            nc.vector.tensor_tensor(
                out=by_col[:, lo:hi, :, 0:PAD, PAD + 1 : 2 * PAD + 1],
                in0=by_col[:, lo:hi, :, 0:PAD, PAD + 1 : 2 * PAD + 1],
                in1=by_col[:, lo:hi, :, 0:PAD, PAD - 1 :: -1],
                op=ALU.add,
            )
            nc.vector.tensor_tensor(
                out=by_col[:, lo:hi, :, SIDE - PAD : SIDE, SIDE - 1 : SIDE + PAD - 1],
                in0=by_col[:, lo:hi, :, SIDE - PAD : SIDE, SIDE - 1 : SIDE + PAD - 1],
                in1=by_col[:, lo:hi, :, SIDE - PAD : SIDE, WIDE - 1 : WIDE - PAD - 1 : -1],
                op=ALU.add,
            )

        fold(0)

        x3_pos = keep.tile([P, SP, HEADS], F32)
        heads_half = N_HALF // SP
        for half in range(HALVES):
            proj = psum.tile([P, N_HALF], F32, tag="proj%d" % half)
            for g in range(PASSES):
                nc.tensor.matmul_mx(
                    out=proj[:],
                    lhsT=x_codes[:, g * P : (g + 1) * P].bitcast(FP8X4),
                    lhsT_scale=x_scales[:, g * P : (g + 1) * P],
                    rhs=w_words[:, g, 2 * N_HALF * half : 2 * N_HALF * (half + 1)].bitcast(FP4X4),
                    rhs_scale=w_scales[:, g, N_HALF * half : N_HALF * (half + 1)],
                    start=(g == 0),
                    stop=(g == PASSES - 1),
                )
            nc.vector.tensor_tensor(
                out=x3_pos[:, :, heads_half * half : heads_half * (half + 1)],
                in0=bias_pos[:, :, heads_half * half : heads_half * (half + 1)],
                in1=proj[:].rearrange("p (h s) -> p s h", s=SP),
                op=ALU.add,
            )

        x3w = keep.tile([P, SIDE, B, SIDE, SP], F32)
        x3_rows = []
        for k in range(SP // PER_BANK):
            x3_head = psum.tile([P, PER_BANK, P], F32, tag="head%d" % k)
            for q in range(PER_BANK):
                nc.tensor.transpose(x3_head[:, q, :], x3_pos[:, PER_BANK * k + q, :], ident[:])
            x3_rows.append(x3_head[:].rearrange("p s (i b j) -> p i b j s", b=B, i=SIDE))
        for k in range(SP // PER_BANK):
            nc.scalar.copy(out=x3w[:, :, :, :, PER_BANK * k : PER_BANK * (k + 1)], in_=x3_rows[k])

        rden = keep.tile([P, B, SIDE, SIDE], F32)
        out_sb = keep.tile([P, B, SP, SIDE, SIDE], F32)
        acc = {}

        def invert(rows):
            nc.vector.reciprocal(out=rden[:, :, rows], in_=den[:, :, rows])

        def weigh(i):
            lo, hi = valid_taps(i)
            rows_in = slice(i + lo - PAD, i + hi - PAD)
            by_tap = e[:, i].rearrange("p d b (j c) -> p d b j c", c=E_PITCH)
            acc[i] = acc_pool.tile([P, P], F32, name="acc")
            blocks = (WIN - 1) * (hi - lo)
            left = [blocks]

            def add_up(block):
                nc.tensor.matmul(
                    out=acc[i][:],
                    lhsT=block.rearrange("p b j s -> p (b j s)"),
                    rhs=ident[:],
                    is_transpose=True,
                    start=(left[0] == blocks),
                    stop=(left[0] == 1),
                )
                left[0] -= 1

            def weights(dx, j_lo, j_hi, width):
                return by_tap[:, lo:hi, :, j_lo:j_hi, dx].unsqueeze(4).to_broadcast([P, hi - lo, B, j_hi - j_lo, width])

            def pool_product(target, dx, j_lo, j_hi):
                nc.gpsimd.tensor_tensor(
                    out=target,
                    in0=x3w[:, rows_in, :, j_lo + dx - PAD : j_hi + dx - PAD, :],
                    in1=weights(dx, j_lo, j_hi, SP),
                    op=ALU.mult,
                )

            first, last = POOL_COLUMNS
            first_lo, first_hi = valid_positions(first)
            last_lo, last_hi = valid_positions(last)
            outer = outer_prods[i % PROD_SETS][:, 0 : hi - lo]
            spare = spare_prods[i % PROD_SETS][:, 0 : hi - lo]
            pool_product(outer[:, :, :, first_lo:first_hi, :], first, first_lo, first_hi)
            pool_product(outer[:, :, :, last_lo:first_lo, :], last, last_lo, first_lo)
            pool_product(spare, last, first_lo, last_hi)
            nc.gpsimd.tensor_tensor(
                out=outer[:, :, :, first_lo:last_hi, :], in0=outer[:, :, :, first_lo:last_hi, :], in1=spare, op=ALU.add
            )
            scalar_from = SCALAR_FROM if i >= SCALAR_FIRST_ROW else SIDE
            for d in range(hi - lo):
                for b in range(B):
                    for j in range(scalar_from, SIDE):
                        nc.scalar.activation(
                            out=prods[SCALAR_COLUMN][i % PROD_SETS][:, d, b, j, :],
                            in_=x3w[:, i + lo + d - PAD, b, j, :],
                            func=ACT.Copy,
                            scale=by_tap[:, lo + d, b, j, SCALAR_COLUMN : SCALAR_COLUMN + 1],
                        )
            for dx in [dx for dx in range(WIN) if dx not in POOL_COLUMNS and dx != SCALAR_COLUMN] + [SCALAR_COLUMN]:
                j_lo, j_hi = valid_positions(dx)
                if dx == SCALAR_COLUMN:
                    j_hi = scalar_from
                for k in range(SP // PER_BANK):
                    nc.vector.tensor_tensor(
                        out=prods[dx][i % PROD_SETS][:, 0 : hi - lo, :, j_lo:j_hi, PER_BANK * k : PER_BANK * (k + 1)],
                        in0=weights(dx, j_lo, j_hi, PER_BANK),
                        in1=x3_rows[k][:, rows_in, :, j_lo + dx - PAD : j_hi + dx - PAD, :],
                        op=ALU.mult,
                    )
                for d in range(hi - lo):
                    add_up(prods[dx][i % PROD_SETS][:, d])
            for d in range(hi - lo):
                add_up(outer[:, d])

        num = {}

        def turn_back(i):
            acc_sb = row_pool.tile([P, P], F32)
            nc.scalar.copy(out=acc_sb[:], in_=acc[i][:])
            if i % 2 == 0:
                num[i // 2] = num_pool.tile([P, B, 2 * SIDE, SP], F32, name="num")
            row = num[i // 2][:, :, SIDE * (i % 2) : SIDE * (i % 2 + 1), :]
            nc.tensor.transpose(row.rearrange("p b j s -> p b (j s)"), acc_sb[:], ident[:])

        def divide(i):
            nc.vector.tensor_tensor(
                out=out_sb[:, :, :, i : i + 2, :].rearrange("p b s i j -> p b s (i j)"),
                in0=rden[:, :, i : i + 2].rearrange("p b i j -> p b (i j)").unsqueeze(2).to_broadcast([P, B, SP, 2 * SIDE]),
                in1=num[i // 2][:].rearrange("p b j s -> p b s j"),
                op=ALU.mult,
            )

        def rows():
            for i in range(SIDE):
                if i + 1 < SIDE:
                    numerators(i + 1)
                weigh(i)
                if i > 0:
                    turn_back(i - 1)
                if i == 2:
                    invert(slice(0, SIDE // 2))
                if i == SIDE // 2 + 2:
                    invert(slice(SIDE // 2, SIDE))
                if i > 0 and i % 2 == 0:
                    divide(i - 2)
                if i + 1 < SIDE:
                    fold(i + 1)
            turn_back(SIDE - 1)
            divide(SIDE - 2)

        rows()

        for b in range(B):
            nc.sync.dma_start(
                out=out[b].rearrange("(h s) i j -> h (s i j)", s=SP),
                in_=out_sb[:, b].rearrange("p s i j -> p (s i j)"),
            )
